import numpy as np
import ml_dtypes


def mxq(x, axis, fmt="e4m3"):
    dtype, down = {"e4m3": (ml_dtypes.float8_e4m3fn, 7), "e5m2": (ml_dtypes.float8_e5m2, 14)}[fmt]
    v = np.moveaxis(np.asarray(x, np.float32).astype(ml_dtypes.bfloat16).astype(np.float64), axis, -1)
    blocks = v.reshape(v.shape[:-1] + (-1, 32))
    amax = np.abs(blocks).max(-1, keepdims=True)
    byte = np.maximum(np.where(amax > 0, np.frexp(amax)[1] - 1 + 127, 0) - down, 1)
    scale = np.exp2(byte - 127.0)
    codes = (blocks / scale).astype(np.float32).astype(dtype).astype(np.float64)
    return np.moveaxis((codes * scale).reshape(v.shape), -1, axis)


WIDE = False


def mx_kscale(k):
    if not WIDE:
        return np.ones(k)
    levels = np.array([18, -18])
    if k % 512:
        return np.exp2(np.random.permutation(np.resize(levels, k // 32))).repeat(32)
    a = np.empty((k // 512, 16))
    for p in range(k // 512):
        a[p, :8] = np.random.permutation(np.resize(levels, 8))
        for g in range(8):
            far = levels[np.abs(levels - a[p, g]) >= 10]
            a[p, g + 8] = far[np.random.randint(len(far))]
    return np.exp2(a.ravel()).repeat(32)


BF16 = ml_dtypes.bfloat16


def bf(x):
    return np.asarray(x, np.float32).astype(BF16)


def f64(x):
    return np.asarray(x).astype(np.float64)


B, N, DIN, DH = 4, 1024, 512, 512


def draw_ahat():
    g = np.random.standard_normal((N, N))
    u = np.random.standard_normal(N) * 0.5
    a = g - g.T + u[:, None] - u[None, :]
    m = (a > 0) + np.eye(N)
    dinv = 1.0 / np.sqrt(m.sum(0))
    return m * (dinv[:, None] * dinv[None, :])


def setup_inputs():
    u = mx_kscale(N)
    v = mx_kscale(DH)
    s = mx_kscale(N)
    r = np.random.standard_normal
    x0 = bf(r((B, N, DIN)).reshape(B * N, DIN))
    ahat0 = bf(draw_ahat())
    w0 = bf(r((DIN, DH)) * 0.2 * np.sqrt(N / DIN))
    b0 = bf(r(DH) * 0.2)
    g = r((B, N, DH)) * np.exp2(np.random.randint(-6, 1, (B, N, 1))) * 16.0
    h = f64(ahat0).T @ (f64(x0) @ f64(w0)).reshape(B, N, DH) + f64(b0)
    return {"x": bf(f64(x0) * np.tile(s, B)[:, None]),
            "ahat": bf(f64(ahat0) / s[:, None] / u[None, :]),
            "gcn1_w": bf(f64(w0) / v[None, :]),
            "gcn1_b": b0,
            "h": np.asarray(h, np.float32),
            "grad_out": bf(g * u[None, :, None] * v[None, None, :])}


def reference(x, ahat, gcn1_w, gcn1_b, h, grad_out):
    dz2 = f64(grad_out) * (f64(h) > 0.0)
    dz1 = mxq(f64(ahat), 1, "e4m3") @ mxq(dz2, 1, "e5m2")
    dz1 = dz1.reshape(B * N, DH)
    dx = mxq(dz1, 1, "e5m2") @ mxq(f64(gcn1_w), 1, "e4m3").T
    dw = mxq(f64(x), 0, "e4m3").T @ mxq(dz1, 0, "e5m2")
    return dx, dw

@@ -1,0 +1,393 @@
+from contextlib import ExitStack
+
+import concourse.mybir as mybir
+from concourse.masks import make_identity
+
+F32 = mybir.dt.float32
+BF16 = mybir.dt.bfloat16
+U32 = mybir.dt.uint32
+U8 = mybir.dt.uint8
+E4M3 = mybir.dt.float8_e4m3fn_x4
+E5M2 = mybir.dt.float8_e5m2_x4
+ALU = mybir.AluOpType
+
+P = 128
+NODES = 1024
+D = 512
+TOKENS = 4096
+UNIT = 512
+UNITS = TOKENS // UNIT
+
+FLOPS = 2 * 4 * NODES * NODES * D + 2 * 2 * TOKENS * D * D
+BYTES = TOKENS * D * 2 + NODES * NODES * 2 + D * D * 2 + TOKENS * D * 6 + TOKENS * D * 4 + D * D * 4
+
+ACT_X = 128
+
+
+def tile_gcn_pb_v_kernel(tc, x, ahat, gcn1_w, gcn1_b, h, grad_out, out_0, out_1):
+    nc = tc.nc
+    h2 = h.rearrange("b n f -> (b n) f")
+    g2 = grad_out.rearrange("b n f -> (b n) f")
+
+    with ExitStack() as ctx:
+        keep = ctx.enter_context(tc.tile_pool(name="keep", bufs=1))
+        pool = ctx.enter_context(tc.tile_pool(name="stream", bufs=3))
+        psum = ctx.enter_context(tc.psum_pool(name="psum", bufs=1))
+
+        ident = keep.tile([P, P], F32, name="ident")
+        make_identity(nc, ident[:])
+        ctx.enter_context(tc.manual_schedule())
+
+        a_codes = []
+        a_scales = []
+        for s in range(2):
+            a_codes.append(keep.tile([P, NODES], U32, name="a_codes%d" % s, align_bytes=64))
+            a_scales.append(keep.tile([P, NODES], U8, name="a_scales%d" % s, align_bytes=64))
+        w_codes = keep.tile([P, D], U32, name="w_codes", align_bytes=64)
+        w_scales = keep.tile([P, D], U8, name="w_scales", align_bytes=64)
+        acc = []
+        for c in range(4):
+            acc.append(psum.tile([P, D], F32, name="acc%d" % c, bufs=1))
+
+        ah = {}
+        wt = {}
+        hg = {}
+        xs = {}
+        zq = {}
+        zc = {}
+        av = {}
+        qv = {}
+        tok = {}
+        gv = {}
+        fc = {}
+        xq = {}
+        xc = {}
+        work = {}
+        ob = {}
+
+        def new_bank():
+            return psum.tile([P, D], F32, name="work", tag="work", bufs=4)
+
+        def codes(key, store, bufs):
+            c = pool.tile([P, D], U32, name=key + "_codes", tag=key + "_codes", bufs=bufs, align_bytes=64)
+            s = pool.tile([P, D], U8, name=key + "_scales", tag=key + "_scales", bufs=bufs, align_bytes=64)
+            return c, s
+
+        def rows(k):
+            return slice(UNIT * k, UNIT * (k + 1))
+
+        def load_ahat(half):
+            t = pool.tile([P, 4, NODES], BF16, name="ahat_rows", tag="ahat_rows", bufs=2, align_bytes=64)
+            view = ahat[rows(half), :].rearrange("(m t) j -> m t j", t=4)
+            nc.sync.dma_start(out=t[:, 0:2, :], in_=view[:, 0:2, :])
+            nc.sync.dma_start(out=t[:, 2:4, :], in_=view[:, 2:4, :])
+            ah[half] = t
+
+        def load_w():
+            t = pool.tile([P, 4, D], BF16, name="w_rows", tag="w_rows", bufs=1, align_bytes=64)
+            nc.sync.dma_start(out=t[:], in_=gcn1_w.rearrange("(d p) f -> p d f", p=P))
+            wt[0] = t
+
+        def load_hg(k, parts=1):
+            ht = pool.tile([P, 4, D], F32, name="h_rows", tag="h_rows", bufs=4, align_bytes=64)
+            gt = pool.tile([P, 4, D], BF16, name="g_rows", tag="g_rows", bufs=4, align_bytes=64)
+            nc.sync.dma_start(out=gt[:], in_=g2[rows(k), :].rearrange("(p j) f -> p j f", j=4))
+            hv = h2[rows(k), :].rearrange("(p j) f -> p j f", j=4)
+            step = D // parts
+            for i in range(parts):
+                cols = slice(i * step, (i + 1) * step)
+                nc.sync.dma_start(out=ht[:, :, cols], in_=hv[:, :, cols])
+            hg[k] = (ht, gt)
+
+        def load_x(k):
+            t = pool.tile([P, 4, D], BF16, name="x_rows", tag="x_rows", bufs=3, align_bytes=64)
+            nc.sync.dma_start(out=t[:], in_=x[rows(k), :].rearrange("(p j) w -> p j w", j=4))
+            xs[k] = t
+
+        def transpose_rows(key, rows_tile, first, pair):
+            bank = new_bank()
+            for i in range(2):
+                words = rows_tile[:, 2 * pair + i, :].bitcast(F32)
+                for u in range(2):
+                    c0 = 256 * i + 128 * u
+                    nc.tensor.transpose(bank[:, c0:c0 + P], words[:, first + u:first + 256:2], ident[:])
+            work[key] = bank
+
+        def empty_transposed(key, pair, dst, engine):
+            out = dst[:, 1024 * pair:1024 * (pair + 1)].bitcast(F32).rearrange("q (t r u) -> q t r u", t=2, u=2)
+            src = work[key][:].rearrange("q (t u r) -> q t r u", t=2, u=2)
+            if engine == "scalar":
+                nc.scalar.copy(out=out, in_=src)
+            else:
+                nc.vector.tensor_copy(out=out, in_=src)
+
+        def new_g(key):
+            gv[key] = pool.tile([P, 4 * D], BF16, name="grouped", tag="grouped", bufs=3, align_bytes=64)
+
+        def ahat_pe(half, s):
+            for pair in range(2):
+                transpose_rows(("a", half, s, pair), ah[half], 256 * s, pair)
+
+        def ahat_empty(half, s):
+            new_g(("a", half, s))
+            for pair in range(2):
+                empty_transposed(("a", half, s, pair), pair, gv[("a", half, s)], "scalar")
+
+        def ahat_quant(half, s):
+            cols = slice(UNIT * half, UNIT * (half + 1))
+            nc.vector.quantize_mx(out=a_codes[s][:, cols].bitcast(E4M3), scales=a_scales[s][:, cols], in_=gv[("a", half, s)][:])
+
+        def w_pe():
+            for pair in range(2):
+                transpose_rows(("w", pair), wt[0], 0, pair)
+
+        def w_empty():
+            new_g("w")
+            for pair in range(2):
+                empty_transposed(("w", pair), pair, gv["w"], "scalar")
+
+        def w_quant():
+            nc.vector.quantize_mx(out=w_codes[:].bitcast(E4M3), scales=w_scales[:], in_=gv["w"][:])
+
+        def z_make(k, f0=0, f1=D):
+            if f0 == 0:
+                zq[k] = pool.tile([P, D, 4], BF16, name="dz2", tag="dz2", bufs=3, align_bytes=64)
+            ht, gt = hg[k]
+            nc.vector.scalar_tensor_tensor(
+                out=zq[k][:, f0:f1, :],
+                in0=ht[:, :, f0:f1].rearrange("p j f -> p f j"),
+                scalar=0.0,
+                in1=gt[:, :, f0:f1].rearrange("p j f -> p f j"),
+                op0=ALU.is_gt,
+                op1=ALU.mult,
+            )
+
+        def z_quant(k, f0=0, f1=D):
+            if f0 == 0:
+                zc[k] = codes("dz2", zc, 4)
+            c, s = zc[k]
+            nc.vector.quantize_mx(out=c[:, f0:f1].bitcast(E5M2), scales=s[:, f0:f1], in_=zq[k][:, f0:f1, :].rearrange("p f j -> p (f j)"))
+
+        def dh_pass(k, t, s):
+            half = k % 2
+            if s == 0:
+                work[("d", k, t)] = new_bank()
+            cols = slice(UNIT * half + P * t, UNIT * half + P * (t + 1))
+            c, sc = zc[k - half + s]
+            nc.tensor.matmul_mx(
+                out=work[("d", k, t)][:],
+                lhsT=a_codes[s][:, cols].bitcast(E4M3), lhsT_scale=a_scales[s][:, cols],
+                rhs=c[:].bitcast(E5M2), rhs_scale=sc[:],
+                start=(s == 0), stop=(s == 1),
+            )
+
+        def dh_empty(k, t):
+            if t == 0:
+                av[k] = pool.tile([P, 4, D], BF16, name="dz1", tag="dz1", bufs=3, align_bytes=64)
+            nc.scalar.copy(
+                out=av[k][:, t, :].rearrange("p (u q e) -> p u q e", u=2, e=2),
+                in_=work[("d", k, t)][:].rearrange("p (q u e) -> p u q e", u=2, e=2),
+            )
+
+        def i_make(k):
+            qv[k] = pool.tile([P, D, 4], BF16, name="dz1_tok", tag="dz1_tok", bufs=2, align_bytes=64)
+            nc.vector.tensor_copy(
+                out=qv[k][:].rearrange("p (c i) t -> p c t i", i=4),
+                in_=av[k][:].rearrange("p t (c i) -> p c t i", i=4),
+            )
+
+        def i_quant(k):
+            tok[k] = codes("tok", tok, 4)
+            c, s = tok[k]
+            nc.vector.quantize_mx(out=c[:].bitcast(E5M2), scales=s[:], in_=qv[k][:].rearrange("p f t -> p (f t)"))
+
+        def tr_pe(k, pair):
+            bank = new_bank()
+            for i in range(2):
+                words = av[k][:, 2 * pair + i, :].bitcast(F32)
+                for u in range(2):
+                    c0 = 256 * i + 128 * u
+                    nc.tensor.transpose(bank[:, c0:c0 + P], words[:, 128 * u:128 * (u + 1)], ident[:])
+            work[("t", k, pair)] = bank
+
+        def tr_empty(k, pair, engine="scalar"):
+            if pair == 0:
+                new_g(("t", k))
+            empty_transposed(("t", k, pair), pair, gv[("t", k)], engine)
+
+        def f_quant(k):
+            fc[k] = codes("feat", fc, 2)
+            c, s = fc[k]
+            nc.vector.quantize_mx(out=c[:].bitcast(E5M2), scales=s[:], in_=gv[("t", k)][:])
+
+        def out0_pe(k, t):
+            bank = new_bank()
+            work[("o", k, t)] = bank
+            c, s = fc[k]
+            cols = slice(P * t, P * (t + 1))
+            nc.tensor.matmul_mx(
+                out=bank[:], lhsT=c[:, cols].bitcast(E5M2), lhsT_scale=s[:, cols],
+                rhs=w_codes[:].bitcast(E4M3), rhs_scale=w_scales[:], start=True, stop=True,
+            )
+
+        def out0_empty(k, t, engine="scalar"):
+            if t == 0:
+                ob[k] = pool.tile([P, 4, D], F32, name="out_rows", tag="out_rows", bufs=3, align_bytes=64)
+            if engine == "scalar":
+                nc.scalar.copy(out=ob[k][:, t, :], in_=work[("o", k, t)][:])
+            else:
+                nc.vector.tensor_copy(out=ob[k][:, t, :], in_=work[("o", k, t)][:])
+
+        def out0_store(k, t0=0, t1=4):
+            view = out_0[rows(k), :].rearrange("(p t) w -> p t w", t=4)
+            nc.sync.dma_start(out=view[:, t0:t1, :], in_=ob[k][:, t0:t1, :])
+
+        def x_make(k):
+            xq[k] = pool.tile([P, D, 4], BF16, name="x_grouped", tag="x_grouped", bufs=2, align_bytes=64)
+            cut = D - ACT_X
+            nc.vector.tensor_copy(
+                out=xq[k][:, 0:cut, :].rearrange("p (c i) j -> p c j i", i=4),
+                in_=xs[k][:, :, 0:cut].rearrange("p j (c i) -> p c j i", i=4),
+            )
+
+        def x_make_act(k):
+            cut = D - ACT_X
+            nc.scalar.copy(
+                out=xq[k][:, cut:D, :].rearrange("p (c i) j -> p c j i", i=4),
+                in_=xs[k][:, :, cut:D].rearrange("p j (c i) -> p c j i", i=4),
+            )
+
+        def x_quant(k):
+            xc[k] = codes("x", xc, 4)
+            c, s = xc[k]
+            nc.vector.quantize_mx(out=c[:].bitcast(E4M3), scales=s[:], in_=xq[k][:].rearrange("p w j -> p (w j)"))
+
+        def out1_pe(k):
+            c, s = xc[k]
+            tc_, ts_ = tok[k]
+            for d in range(4):
+                cols = slice(P * d, P * (d + 1))
+                nc.tensor.matmul_mx(
+                    out=acc[d][:], lhsT=c[:, cols].bitcast(E4M3), lhsT_scale=s[:, cols],
+                    rhs=tc_[:].bitcast(E5M2), rhs_scale=ts_[:], start=(k == 0), stop=(k == UNITS - 1),
+                )
+
+        load_ahat(0)
+        load_hg(0)
+        load_hg(1, parts=2)
+        load_hg(2)
+        load_ahat(1)
+        load_w()
+        load_hg(3)
+        load_x(0)
+
+        ahat_pe(0, 0)
+        ahat_pe(0, 1)
+        ahat_empty(0, 0)
+        ahat_empty(0, 1)
+        ahat_quant(0, 0)
+        ahat_quant(0, 1)
+        z_make(0)
+        load_hg(4)
+        load_x(1)
+        z_make(1, 0, 256)
+        z_quant(0)
+        z_make(1, 256, 512)
+        load_hg(5)
+        load_x(2)
+        z_quant(1, 0, 256)
+        z_quant(1, 256, 512)
+
+        for k in range(UNITS):
+            xk = [[], [0], [1], [2], [3], [4], [5, 6], [7]][k]
+            if k == 0:
+                for s in range(2):
+                    for t in range(4):
+                        dh_pass(k, t, s)
+            else:
+                for t in range(4):
+                    dh_pass(k, t, 0)
+                    dh_pass(k, t, 1)
+            for t in range(4):
+                dh_empty(k, t)
+            if k > 0:
+                f_quant(k - 1)
+            if k + 2 < UNITS:
+                z_make(k + 2)
+                if k + 6 < UNITS:
+                    load_hg(k + 6)
+            if k == 0:
+                ahat_pe(1, 0)
+                ahat_pe(1, 1)
+                ahat_empty(1, 0)
+                ahat_empty(1, 1)
+                w_pe()
+                w_empty()
+                i_make(0)
+                ahat_quant(1, 0)
+                z_quant(2)
+                ahat_quant(1, 1)
+                w_quant()
+                i_quant(0)
+                tr_pe(0, 0)
+                tr_pe(0, 1)
+                tr_empty(0, 0)
+                tr_empty(0, 1)
+                continue
+            for t in range(4):
+                out0_pe(k - 1, t)
+            for t in range(4):
+                out0_empty(k - 1, t)
+            out0_store(k - 1)
+            if k >= 2:
+                out1_pe(k - 2)
+            tr_pe(k, 0)
+            tr_pe(k, 1)
+            tr_empty(k, 0)
+            tr_empty(k, 1)
+            if k + 2 < UNITS:
+                i_make(k)
+                z_quant(k + 2)
+                x_make(xk[0])
+                x_make_act(xk[0])
+                i_quant(k)
+                x_quant(xk[0])
+                if k + 2 < UNITS and xk[0] + 3 < UNITS:
+                    load_x(xk[0] + 3)
+            elif k == 6:
+                x_make(xk[0])
+                x_make_act(xk[0])
+                i_make(k)
+                x_quant(xk[0])
+                x_make(xk[1])
+                x_make_act(xk[1])
+                i_quant(k)
+                x_quant(xk[1])
+            else:
+                x_make(xk[0])
+                x_make_act(xk[0])
+                i_make(k)
+                x_quant(xk[0])
+                i_quant(k)
+
+        last = UNITS - 1
+        f_quant(last)
+        out1_pe(last - 1)
+        out1_pe(last)
+        for t in range(4):
+            out0_pe(last, t)
+        o1 = keep.tile([P, 4, D], F32, name="out1_rows", align_bytes=64)
+        for d in range(4):
+            dst = o1[:, d, :].rearrange("p (q u e) -> p q u e", u=2, e=2)
+            srcv = acc[d][:].rearrange("p (u q e) -> p q u e", u=2, e=2)
+            if d % 2 == 0:
+                nc.scalar.copy(out=dst, in_=srcv)
+            else:
+                nc.vector.tensor_copy(out=dst, in_=srcv)
+        o1view = out_1.rearrange("(d p) f -> p d f", p=P)
+        nc.sync.dma_start(out=o1view[:, 0:2, :], in_=o1[:, 0:2, :])
+        nc.sync.dma_start(out=o1view[:, 2:4, :], in_=o1[:, 2:4, :])
+        for t in range(4):
+            out0_empty(last, t, "scalar" if t % 2 == 0 else "vector")
+            if t % 2 == 1:
+                out0_store(last, t - 1, t + 1)

@@ -21,7 +21,8 @@ UNITS = TOKENS // UNIT
 FLOPS = 2 * 4 * NODES * NODES * D + 2 * 2 * TOKENS * D * D
 BYTES = TOKENS * D * 2 + NODES * NODES * 2 + D * D * 2 + TOKENS * D * 6 + TOKENS * D * 4 + D * D * 4
 
-ACT_X = 128
+S = "scalar"
+V = "vector"
 
 
 def tile_gcn_pb_v_kernel(tc, x, ahat, gcn1_w, gcn1_b, h, grad_out, out_0, out_1):
@@ -36,6 +37,8 @@ def tile_gcn_pb_v_kernel(tc, x, ahat, gcn1_w, gcn1_b, h, grad_out, out_0, out_1)
 
         ident = keep.tile([P, P], F32, name="ident")
         make_identity(nc, ident[:])
+        ident_bf = keep.tile([P, P], BF16, name="ident_bf")
+        make_identity(nc, ident_bf[:])
         ctx.enter_context(tc.manual_schedule())
 
         a_codes = []
@@ -45,30 +48,18 @@ def tile_gcn_pb_v_kernel(tc, x, ahat, gcn1_w, gcn1_b, h, grad_out, out_0, out_1)
             a_scales.append(keep.tile([P, NODES], U8, name="a_scales%d" % s, align_bytes=64))
         w_codes = keep.tile([P, D], U32, name="w_codes", align_bytes=64)
         w_scales = keep.tile([P, D], U8, name="w_scales", align_bytes=64)
+        o1 = keep.tile([P, 4, D], F32, name="out1_rows", align_bytes=64)
         acc = []
         for c in range(4):
             acc.append(psum.tile([P, D], F32, name="acc%d" % c, bufs=1))
 
-        ah = {}
-        wt = {}
-        hg = {}
-        xs = {}
-        zq = {}
-        zc = {}
-        av = {}
-        qv = {}
-        tok = {}
-        gv = {}
-        fc = {}
-        xq = {}
-        xc = {}
-        work = {}
-        ob = {}
+        ah, wt, hg, xs, zt, zc, av, qv, tok, gv, fc, xt, xc, work, ob = {}, {}, {}, {}, {}, {}, {}, {}, {}, {}, {}, {}, {}, {}, {}
+        o1view = out_1.rearrange("(d p) f -> p d f", p=P)
 
         def new_bank():
             return psum.tile([P, D], F32, name="work", tag="work", bufs=4)
 
-        def codes(key, store, bufs):
+        def codes(key, bufs):
             c = pool.tile([P, D], U32, name=key + "_codes", tag=key + "_codes", bufs=bufs, align_bytes=64)
             s = pool.tile([P, D], U8, name=key + "_scales", tag=key + "_scales", bufs=bufs, align_bytes=64)
             return c, s
@@ -76,35 +67,37 @@ def tile_gcn_pb_v_kernel(tc, x, ahat, gcn1_w, gcn1_b, h, grad_out, out_0, out_1)
         def rows(k):
             return slice(UNIT * k, UNIT * (k + 1))
 
-        def load_ahat(half):
-            t = pool.tile([P, 4, NODES], BF16, name="ahat_rows", tag="ahat_rows", bufs=2, align_bytes=64)
+        def copy(engine, out, in_):
+            if engine == S:
+                nc.scalar.copy(out=out, in_=in_)
+            else:
+                nc.vector.tensor_copy(out=out, in_=in_)
+
+        def la(half, pair):
+            if half not in ah:
+                ah[half] = pool.tile([P, 4, NODES], BF16, name="ahat_rows", tag="ahat_rows", bufs=2, align_bytes=64)
             view = ahat[rows(half), :].rearrange("(m t) j -> m t j", t=4)
-            nc.sync.dma_start(out=t[:, 0:2, :], in_=view[:, 0:2, :])
-            nc.sync.dma_start(out=t[:, 2:4, :], in_=view[:, 2:4, :])
-            ah[half] = t
+            nc.sync.dma_start(out=ah[half][:, 2 * pair:2 * pair + 2, :], in_=view[:, 2 * pair:2 * pair + 2, :])
 
-        def load_w():
-            t = pool.tile([P, 4, D], BF16, name="w_rows", tag="w_rows", bufs=1, align_bytes=64)
-            nc.sync.dma_start(out=t[:], in_=gcn1_w.rearrange("(d p) f -> p d f", p=P))
-            wt[0] = t
+        def lw():
+            wt[0] = pool.tile([P, 4, D], BF16, name="w_rows", tag="w_rows", bufs=1, align_bytes=64)
+            nc.sync.dma_start(out=wt[0][:], in_=gcn1_w.rearrange("(d p) f -> p d f", p=P))
 
-        def load_hg(k, parts=1):
-            ht = pool.tile([P, 4, D], F32, name="h_rows", tag="h_rows", bufs=4, align_bytes=64)
-            gt = pool.tile([P, 4, D], BF16, name="g_rows", tag="g_rows", bufs=4, align_bytes=64)
-            nc.sync.dma_start(out=gt[:], in_=g2[rows(k), :].rearrange("(p j) f -> p j f", j=4))
-            hv = h2[rows(k), :].rearrange("(p j) f -> p j f", j=4)
-            step = D // parts
-            for i in range(parts):
-                cols = slice(i * step, (i + 1) * step)
-                nc.sync.dma_start(out=ht[:, :, cols], in_=hv[:, :, cols])
-            hg[k] = (ht, gt)
+        def lg(k, c0=0, c1=D):
+            if ("g", k) not in hg:
+                hg["g", k] = pool.tile([P, 4, D], BF16, name="g_rows", tag="g_rows", bufs=4, align_bytes=64)
+            nc.sync.dma_start(out=hg["g", k][:, :, c0:c1], in_=g2[rows(k), c0:c1].rearrange("(p j) f -> p j f", j=4))
 
-        def load_x(k):
-            t = pool.tile([P, 4, D], BF16, name="x_rows", tag="x_rows", bufs=3, align_bytes=64)
-            nc.sync.dma_start(out=t[:], in_=x[rows(k), :].rearrange("(p j) w -> p j w", j=4))
-            xs[k] = t
+        def lh(k, c0=0, c1=D):
+            if ("h", k) not in hg:
+                hg["h", k] = pool.tile([P, 4, D], F32, name="h_rows", tag="h_rows", bufs=4, align_bytes=64)
+            nc.sync.dma_start(out=hg["h", k][:, :, c0:c1], in_=h2[rows(k), c0:c1].rearrange("(p j) f -> p j f", j=4))
 
-        def transpose_rows(key, rows_tile, first, pair):
+        def lx(k):
+            xs[k] = pool.tile([P, 4, D], BF16, name="x_rows", tag="x_rows", bufs=3, align_bytes=64)
+            nc.sync.dma_start(out=xs[k][:], in_=x[rows(k), :].rearrange("(p j) w -> p j w", j=4))
+
+        def every_second(key, rows_tile, first, pair):
             bank = new_bank()
             for i in range(2):
                 words = rows_tile[:, 2 * pair + i, :].bitcast(F32)
@@ -113,116 +106,101 @@ def tile_gcn_pb_v_kernel(tc, x, ahat, gcn1_w, gcn1_b, h, grad_out, out_0, out_1)
                     nc.tensor.transpose(bank[:, c0:c0 + P], words[:, first + u:first + 256:2], ident[:])
             work[key] = bank
 
-        def empty_transposed(key, pair, dst, engine):
-            out = dst[:, 1024 * pair:1024 * (pair + 1)].bitcast(F32).rearrange("q (t r u) -> q t r u", t=2, u=2)
-            src = work[key][:].rearrange("q (t u r) -> q t r u", t=2, u=2)
-            if engine == "scalar":
-                nc.scalar.copy(out=out, in_=src)
-            else:
-                nc.vector.tensor_copy(out=out, in_=src)
+        def turned_out(key, gkey, pair, engine):
+            if gkey not in gv:
+                gv[gkey] = pool.tile([P, 4 * D], BF16, name="grouped", tag="grouped", bufs=4, align_bytes=64)
+            out = gv[gkey][:, 1024 * pair:1024 * (pair + 1)].bitcast(F32).rearrange("q (t r u) -> q t r u", t=2, u=2)
+            copy(engine, out, work[key][:].rearrange("q (t u r) -> q t r u", t=2, u=2))
 
-        def new_g(key):
-            gv[key] = pool.tile([P, 4 * D], BF16, name="grouped", tag="grouped", bufs=3, align_bytes=64)
+        def at(half, s, pair):
+            every_second(("a", half, s, pair), ah[half], 256 * s, pair)
 
-        def ahat_pe(half, s):
-            for pair in range(2):
-                transpose_rows(("a", half, s, pair), ah[half], 256 * s, pair)
+        def ae(half, s, pair, engine):
+            turned_out(("a", half, s, pair), ("a", half, s), pair, engine)
 
-        def ahat_empty(half, s):
-            new_g(("a", half, s))
-            for pair in range(2):
-                empty_transposed(("a", half, s, pair), pair, gv[("a", half, s)], "scalar")
+        def aq(half, s, pair):
+            cols = slice(UNIT * half + 256 * pair, UNIT * half + 256 * (pair + 1))
+            src = gv["a", half, s][:, 1024 * pair:1024 * (pair + 1)]
+            nc.vector.quantize_mx(out=a_codes[s][:, cols].bitcast(E4M3), scales=a_scales[s][:, cols], in_=src)
 
-        def ahat_quant(half, s):
-            cols = slice(UNIT * half, UNIT * (half + 1))
-            nc.vector.quantize_mx(out=a_codes[s][:, cols].bitcast(E4M3), scales=a_scales[s][:, cols], in_=gv[("a", half, s)][:])
+        def wtr(pair):
+            every_second(("w", pair), wt[0], 0, pair)
 
-        def w_pe():
-            for pair in range(2):
-                transpose_rows(("w", pair), wt[0], 0, pair)
+        def we(pair, engine):
+            turned_out(("w", pair), "w", pair, engine)
 
-        def w_empty():
-            new_g("w")
-            for pair in range(2):
-                empty_transposed(("w", pair), pair, gv["w"], "scalar")
-
-        def w_quant():
+        def wq():
             nc.vector.quantize_mx(out=w_codes[:].bitcast(E4M3), scales=w_scales[:], in_=gv["w"][:])
 
-        def z_make(k, f0=0, f1=D):
-            if f0 == 0:
-                zq[k] = pool.tile([P, D, 4], BF16, name="dz2", tag="dz2", bufs=3, align_bytes=64)
-            ht, gt = hg[k]
+        def z(k, f0=0, f1=D):
+            if k not in zt:
+                zt[k] = pool.tile([P, D, 4], BF16, name="dz2", tag="dz2", bufs=3, align_bytes=64)
             nc.vector.scalar_tensor_tensor(
-                out=zq[k][:, f0:f1, :],
-                in0=ht[:, :, f0:f1].rearrange("p j f -> p f j"),
+                out=zt[k][:, f0:f1, :],
+                in0=hg["h", k][:, :, f0:f1].rearrange("p j f -> p f j"),
                 scalar=0.0,
-                in1=gt[:, :, f0:f1].rearrange("p j f -> p f j"),
+                in1=hg["g", k][:, :, f0:f1].rearrange("p j f -> p f j"),
                 op0=ALU.is_gt,
                 op1=ALU.mult,
             )
 
-        def z_quant(k, f0=0, f1=D):
-            if f0 == 0:
-                zc[k] = codes("dz2", zc, 4)
+        def zq(k, f0=0, f1=D):
+            if k not in zc:
+                zc[k] = codes("dz2", 4)
             c, s = zc[k]
-            nc.vector.quantize_mx(out=c[:, f0:f1].bitcast(E5M2), scales=s[:, f0:f1], in_=zq[k][:, f0:f1, :].rearrange("p f j -> p (f j)"))
+            nc.vector.quantize_mx(out=c[:, f0:f1].bitcast(E5M2), scales=s[:, f0:f1], in_=zt[k][:, f0:f1, :].rearrange("p f j -> p (f j)"))
 
-        def dh_pass(k, t, s):
+        def dh(k, t):
             half = k % 2
-            if s == 0:
-                work[("d", k, t)] = new_bank()
+            work["d", k, t] = new_bank()
             cols = slice(UNIT * half + P * t, UNIT * half + P * (t + 1))
-            c, sc = zc[k - half + s]
-            nc.tensor.matmul_mx(
-                out=work[("d", k, t)][:],
-                lhsT=a_codes[s][:, cols].bitcast(E4M3), lhsT_scale=a_scales[s][:, cols],
-                rhs=c[:].bitcast(E5M2), rhs_scale=sc[:],
-                start=(s == 0), stop=(s == 1),
-            )
+            for s in range(2):
+                c, sc = zc[k - half + s]
+                nc.tensor.matmul_mx(
+                    out=work["d", k, t][:],
+                    lhsT=a_codes[s][:, cols].bitcast(E4M3), lhsT_scale=a_scales[s][:, cols],
+                    rhs=c[:].bitcast(E5M2), rhs_scale=sc[:],
+                    start=(s == 0), stop=(s == 1),
+                )
 
-        def dh_empty(k, t):
-            if t == 0:
+        def de(k, t, engine):
+            if k not in av:
                 av[k] = pool.tile([P, 4, D], BF16, name="dz1", tag="dz1", bufs=3, align_bytes=64)
-            nc.scalar.copy(
-                out=av[k][:, t, :].rearrange("p (u q e) -> p u q e", u=2, e=2),
-                in_=work[("d", k, t)][:].rearrange("p (q u e) -> p u q e", u=2, e=2),
-            )
+            copy(engine, av[k][:, t, :].rearrange("p (u q e) -> p u q e", u=2, e=2),
+                 work["d", k, t][:].rearrange("p (q u e) -> p u q e", u=2, e=2))
 
-        def i_make(k):
+        def im(k):
             qv[k] = pool.tile([P, D, 4], BF16, name="dz1_tok", tag="dz1_tok", bufs=2, align_bytes=64)
             nc.vector.tensor_copy(
                 out=qv[k][:].rearrange("p (c i) t -> p c t i", i=4),
                 in_=av[k][:].rearrange("p t (c i) -> p c t i", i=4),
             )
 
-        def i_quant(k):
-            tok[k] = codes("tok", tok, 4)
+        def iq(k):
+            tok[k] = codes("tok", 4)
             c, s = tok[k]
             nc.vector.quantize_mx(out=c[:].bitcast(E5M2), scales=s[:], in_=qv[k][:].rearrange("p f t -> p (f t)"))
 
-        def tr_pe(k, pair):
+        def tr(k, pair):
             bank = new_bank()
             for i in range(2):
                 words = av[k][:, 2 * pair + i, :].bitcast(F32)
                 for u in range(2):
                     c0 = 256 * i + 128 * u
                     nc.tensor.transpose(bank[:, c0:c0 + P], words[:, 128 * u:128 * (u + 1)], ident[:])
-            work[("t", k, pair)] = bank
+            work["t", k, pair] = bank
 
-        def tr_empty(k, pair, engine="scalar"):
-            if pair == 0:
-                new_g(("t", k))
-            empty_transposed(("t", k, pair), pair, gv[("t", k)], engine)
+        def te(k, pair, engine):
+            turned_out(("t", k, pair), ("t", k), pair, engine)
 
-        def f_quant(k):
-            fc[k] = codes("feat", fc, 2)
+        def fq(k):
+            fc[k] = codes("feat", 2)
             c, s = fc[k]
-            nc.vector.quantize_mx(out=c[:].bitcast(E5M2), scales=s[:], in_=gv[("t", k)][:])
+            nc.vector.quantize_mx(out=c[:].bitcast(E5M2), scales=s[:], in_=gv["t", k][:])
 
-        def out0_pe(k, t):
+        def o0(k, t):
             bank = new_bank()
-            work[("o", k, t)] = bank
+            work["o", k, t] = bank
             c, s = fc[k]
             cols = slice(P * t, P * (t + 1))
             nc.tensor.matmul_mx(
@@ -230,164 +208,400 @@ def tile_gcn_pb_v_kernel(tc, x, ahat, gcn1_w, gcn1_b, h, grad_out, out_0, out_1)
                 rhs=w_codes[:].bitcast(E4M3), rhs_scale=w_scales[:], start=True, stop=True,
             )
 
-        def out0_empty(k, t, engine="scalar"):
-            if t == 0:
+        def oe(k, t, engine):
+            if k not in ob:
                 ob[k] = pool.tile([P, 4, D], F32, name="out_rows", tag="out_rows", bufs=3, align_bytes=64)
-            if engine == "scalar":
-                nc.scalar.copy(out=ob[k][:, t, :], in_=work[("o", k, t)][:])
-            else:
-                nc.vector.tensor_copy(out=ob[k][:, t, :], in_=work[("o", k, t)][:])
+            copy(engine, ob[k][:, t, :], work["o", k, t][:])
 
-        def out0_store(k, t0=0, t1=4):
+        def st(k, t0=0, t1=4):
             view = out_0[rows(k), :].rearrange("(p t) w -> p t w", t=4)
             nc.sync.dma_start(out=view[:, t0:t1, :], in_=ob[k][:, t0:t1, :])
 
-        def x_make(k):
-            xq[k] = pool.tile([P, D, 4], BF16, name="x_grouped", tag="x_grouped", bufs=2, align_bytes=64)
-            cut = D - ACT_X
-            nc.vector.tensor_copy(
-                out=xq[k][:, 0:cut, :].rearrange("p (c i) j -> p c j i", i=4),
-                in_=xs[k][:, :, 0:cut].rearrange("p j (c i) -> p c j i", i=4),
-            )
-
-        def x_make_act(k):
-            cut = D - ACT_X
-            nc.scalar.copy(
-                out=xq[k][:, cut:D, :].rearrange("p (c i) j -> p c j i", i=4),
-                in_=xs[k][:, :, cut:D].rearrange("p j (c i) -> p c j i", i=4),
-            )
-
-        def x_quant(k):
-            xc[k] = codes("x", xc, 4)
-            c, s = xc[k]
-            nc.vector.quantize_mx(out=c[:].bitcast(E4M3), scales=s[:], in_=xq[k][:].rearrange("p w j -> p (w j)"))
-
-        def out1_pe(k):
-            c, s = xc[k]
-            tc_, ts_ = tok[k]
-            for d in range(4):
-                cols = slice(P * d, P * (d + 1))
-                nc.tensor.matmul_mx(
-                    out=acc[d][:], lhsT=c[:, cols].bitcast(E4M3), lhsT_scale=s[:, cols],
-                    rhs=tc_[:].bitcast(E5M2), rhs_scale=ts_[:], start=(k == 0), stop=(k == UNITS - 1),
+        def xp(k, half):
+            bank = psum.tile([P, 2 * D], BF16, name="xbank", tag="work", bufs=4)
+            for q in range(2):
+                cols = slice(256 * half + 128 * q, 256 * half + 128 * (q + 1))
+                nc.tensor.matmul(
+                    out=bank[:, 512 * q:512 * (q + 1)],
+                    lhsT=ident_bf[:],
+                    rhs=xs[k][:, :, cols].rearrange("p j w -> p w j"),
+                    start=True, stop=True,
                 )
+            work["x", k, half] = bank
 
-        load_ahat(0)
-        load_hg(0)
-        load_hg(1, parts=2)
-        load_hg(2)
-        load_ahat(1)
-        load_w()
-        load_hg(3)
-        load_x(0)
+        def new_xt(k):
+            if k not in xt:
+                xt[k] = pool.tile([P, D, 4], BF16, name="x_grouped", tag="x_grouped", bufs=2, align_bytes=64)
+            return xt[k]
 
-        ahat_pe(0, 0)
-        ahat_pe(0, 1)
-        ahat_empty(0, 0)
-        ahat_empty(0, 1)
-        ahat_quant(0, 0)
-        ahat_quant(0, 1)
-        z_make(0)
-        load_hg(4)
-        load_x(1)
-        z_make(1, 0, 256)
-        z_quant(0)
-        z_make(1, 256, 512)
-        load_hg(5)
-        load_x(2)
-        z_quant(1, 0, 256)
-        z_quant(1, 256, 512)
+        def xe(k, half, engine):
+            out = new_xt(k)[:, 256 * half:256 * (half + 1), :].rearrange("p w j -> p (w j)")
+            copy(engine, out, work["x", k, half][:])
 
-        for k in range(UNITS):
-            xk = [[], [0], [1], [2], [3], [4], [5, 6], [7]][k]
-            if k == 0:
-                for s in range(2):
-                    for t in range(4):
-                        dh_pass(k, t, s)
-            else:
-                for t in range(4):
-                    dh_pass(k, t, 0)
-                    dh_pass(k, t, 1)
-            for t in range(4):
-                dh_empty(k, t)
-            if k > 0:
-                f_quant(k - 1)
-            if k + 2 < UNITS:
-                z_make(k + 2)
-                if k + 6 < UNITS:
-                    load_hg(k + 6)
-            if k == 0:
-                ahat_pe(1, 0)
-                ahat_pe(1, 1)
-                ahat_empty(1, 0)
-                ahat_empty(1, 1)
-                w_pe()
-                w_empty()
-                i_make(0)
-                ahat_quant(1, 0)
-                z_quant(2)
-                ahat_quant(1, 1)
-                w_quant()
-                i_quant(0)
-                tr_pe(0, 0)
-                tr_pe(0, 1)
-                tr_empty(0, 0)
-                tr_empty(0, 1)
-                continue
-            for t in range(4):
-                out0_pe(k - 1, t)
-            for t in range(4):
-                out0_empty(k - 1, t)
-            out0_store(k - 1)
-            if k >= 2:
-                out1_pe(k - 2)
-            tr_pe(k, 0)
-            tr_pe(k, 1)
-            tr_empty(k, 0)
-            tr_empty(k, 1)
-            if k + 2 < UNITS:
-                i_make(k)
-                z_quant(k + 2)
-                x_make(xk[0])
-                x_make_act(xk[0])
-                i_quant(k)
-                x_quant(xk[0])
-                if k + 2 < UNITS and xk[0] + 3 < UNITS:
-                    load_x(xk[0] + 3)
-            elif k == 6:
-                x_make(xk[0])
-                x_make_act(xk[0])
-                i_make(k)
-                x_quant(xk[0])
-                x_make(xk[1])
-                x_make_act(xk[1])
-                i_quant(k)
-                x_quant(xk[1])
-            else:
-                x_make(xk[0])
-                x_make_act(xk[0])
-                i_make(k)
-                x_quant(xk[0])
-                i_quant(k)
+        def xm(k, c0, c1, engine):
+            copy(engine, new_xt(k)[:, c0:c1, :].rearrange("p (c i) j -> p c j i", i=4),
+                 xs[k][:, :, c0:c1].rearrange("p j (c i) -> p c j i", i=4))
 
-        last = UNITS - 1
-        f_quant(last)
-        out1_pe(last - 1)
-        out1_pe(last)
-        for t in range(4):
-            out0_pe(last, t)
-        o1 = keep.tile([P, 4, D], F32, name="out1_rows", align_bytes=64)
-        for d in range(4):
-            dst = o1[:, d, :].rearrange("p (q u e) -> p q u e", u=2, e=2)
-            srcv = acc[d][:].rearrange("p (u q e) -> p q u e", u=2, e=2)
-            if d % 2 == 0:
-                nc.scalar.copy(out=dst, in_=srcv)
-            else:
-                nc.vector.tensor_copy(out=dst, in_=srcv)
-        o1view = out_1.rearrange("(d p) f -> p d f", p=P)
-        nc.sync.dma_start(out=o1view[:, 0:2, :], in_=o1[:, 0:2, :])
-        nc.sync.dma_start(out=o1view[:, 2:4, :], in_=o1[:, 2:4, :])
-        for t in range(4):
-            out0_empty(last, t, "scalar" if t % 2 == 0 else "vector")
-            if t % 2 == 1:
-                out0_store(last, t - 1, t + 1)
+        def xq(k):
+            xc[k] = codes("x", 4)
+            c, s = xc[k]
+            nc.vector.quantize_mx(out=c[:].bitcast(E4M3), scales=s[:], in_=xt[k][:].rearrange("p w j -> p (w j)"))
+
+        def o1p(k, d):
+            xcod, xsc = xc[k]
+            tcod, tsc = tok[k]
+            cols = slice(P * d, P * (d + 1))
+            nc.tensor.matmul_mx(
+                out=acc[d][:], lhsT=xcod[:, cols].bitcast(E4M3), lhsT_scale=xsc[:, cols],
+                rhs=tcod[:].bitcast(E5M2), rhs_scale=tsc[:], start=(k == 0), stop=(k == UNITS - 1),
+            )
+
+        def pe(d, engine):
+            copy(engine, o1[:, d, :].rearrange("p (q u e) -> p q u e", u=2, e=2),
+                 acc[d][:].rearrange("p (u q e) -> p q u e", u=2, e=2))
+
+        def sp(d0, d1):
+            nc.sync.dma_start(out=o1view[:, d0:d1, :], in_=o1[:, d0:d1, :])
+
+        lg(0, 256, 512)
+        lh(0, 256, 512)
+        la(0, 0)
+        lg(0, 0, 256)
+        lh(0, 0, 256)
+        z(0, 256, 512)
+        lh(1, 0, 256)
+        z(0, 0, 256)
+        at(0, 1, 0)
+        at(0, 0, 0)
+        ae(0, 1, 0, S)
+        lg(1)
+        zq(0)
+        la(0, 1)
+        lh(1, 256, 512)
+        z(1, 0, 256)
+        zq(1, 0, 256)
+        at(0, 1, 1)
+        ae(0, 1, 1, S)
+        at(0, 0, 1)
+        lg(2)
+        ae(0, 0, 0, S)
+        lh(2)
+        ae(0, 0, 1, S)
+        z(1, 256, 512)
+        aq(0, 0, 0)
+        zq(1, 256, 512)
+        aq(0, 1, 0)
+        aq(0, 0, 1)
+        la(1, 0)
+        dh(0, 1)
+        aq(0, 1, 1)
+        la(1, 1)
+        de(0, 1, S)
+        dh(0, 3)
+        de(0, 3, S)
+        z(2, 0, 256)
+        dh(0, 0)
+        dh(0, 2)
+        de(0, 0, S)
+        lw()
+        z(2, 256, 512)
+        at(1, 0, 0)
+        at(1, 1, 1)
+        tr(0, 0)
+        de(0, 2, S)
+        lh(3)
+        ae(1, 0, 0, S)
+        at(1, 0, 1)
+        tr(0, 1)
+        im(0)
+        ae(1, 1, 1, S)
+        te(0, 0, S)
+        at(1, 1, 0)
+        aq(1, 1, 1)
+        wtr(0)
+        ae(1, 0, 1, S)
+        iq(0)
+        zq(2)
+        ae(1, 1, 0, S)
+        te(0, 1, S)
+        aq(1, 0, 0)
+        aq(1, 1, 0)
+        wtr(1)
+        we(1, S)
+        lx(0)
+        aq(1, 0, 1)
+        we(0, S)
+        dh(1, 1)
+        xm(0, 256, 512, S)
+        fq(0)
+        dh(1, 0)
+        xm(0, 0, 256, V)
+        de(1, 1, S)
+        wq()
+        dh(1, 3)
+        de(1, 0, S)
+        lg(3)
+        o0(0, 3)
+        lx(1)
+        de(1, 3, S)
+        z(3, 256, 512)
+        o0(0, 2)
+        oe(0, 3, S)
+        lg(4)
+        dh(1, 2)
+        de(1, 2, S)
+        z(3, 0, 256)
+        xm(1, 256, 512, V)
+        lx(2)
+        o0(0, 0)
+        oe(0, 2, S)
+        zq(3)
+        tr(1, 1)
+        tr(1, 0)
+        oe(0, 0, S)
+        te(1, 1, S)
+        xm(1, 0, 256, V)
+        im(1)
+        o0(0, 1)
+        dh(2, 0)
+        te(1, 0, S)
+        fq(1)
+        lh(5)
+        xq(0)
+        lg(5)
+        dh(2, 2)
+        lg(7)
+        oe(0, 1, S)
+        dh(2, 3)
+        lh(4)
+        dh(2, 1)
+        de(2, 0, S)
+        de(2, 2, S)
+        de(2, 3, S)
+        de(2, 1, S)
+        lx(3)
+        z(5, 0, 256)
+        o0(1, 0)
+        iq(1)
+        lh(7)
+        o0(1, 3)
+        oe(1, 0, S)
+        o0(1, 1)
+        tr(2, 0)
+        dh(3, 0)
+        xq(1)
+        lx(4)
+        z(5, 256, 512)
+        xm(2, 0, 256, S)
+        o1p(0, 3)
+        oe(1, 3, S)
+        o1p(0, 0)
+        lg(6)
+        o1p(1, 3)
+        z(4, 256, 512)
+        o0(1, 2)
+        oe(1, 1, S)
+        te(2, 0, S)
+        dh(3, 1)
+        z(4, 0, 256)
+        de(3, 0, S)
+        lh(6)
+        o1p(0, 1)
+        im(2)
+        tr(2, 1)
+        oe(1, 2, S)
+        o1p(0, 2)
+        dh(3, 3)
+        de(3, 1, S)
+        te(2, 1, S)
+        dh(3, 2)
+        fq(2)
+        de(3, 3, S)
+        zq(4)
+        de(3, 2, S)
+        o1p(1, 0)
+        tr(3, 1)
+        o0(2, 3)
+        xm(3, 256, 512, S)
+        zq(5)
+        te(3, 1, S)
+        tr(3, 0)
+        xm(2, 256, 512, S)
+        z(6, 0, 256)
+        o0(2, 0)
+        te(3, 0, S)
+        st(0)
+        oe(2, 3, S)
+        oe(2, 0, S)
+        o0(2, 1)
+        dh(4, 1)
+        xq(2)
+        fq(3)
+        oe(2, 1, S)
+        o0(2, 2)
+        dh(4, 0)
+        de(4, 1, S)
+        o0(3, 3)
+        oe(2, 2, S)
+        oe(3, 3, S)
+        o0(3, 1)
+        im(3)
+        xm(3, 0, 256, V)
+        de(4, 0, S)
+        oe(3, 1, S)
+        o1p(1, 1)
+        iq(2)
+        dh(4, 2)
+        o1p(1, 2)
+        z(6, 256, 512)
+        o0(3, 0)
+        oe(3, 0, S)
+        dh(4, 3)
+        z(7, 256, 512)
+        tr(4, 0)
+        de(4, 2, S)
+        de(4, 3, S)
+        z(7, 0, 256)
+        te(4, 0, S)
+        lx(5)
+        st(1)
+        zq(6)
+        tr(4, 1)
+        xq(3)
+        te(4, 1, S)
+        o0(3, 2)
+        xm(4, 256, 512, S)
+        dh(5, 3)
+        dh(5, 2)
+        fq(4)
+        iq(3)
+        o1p(2, 2)
+        de(5, 3, S)
+        zq(7)
+        dh(5, 1)
+        xm(5, 0, 256, V)
+        oe(3, 2, S)
+        de(5, 2, S)
+        de(5, 1, S)
+        xm(5, 256, 512, S)
+        dh(5, 0)
+        tr(5, 1)
+        o0(4, 2)
+        xm(4, 0, 256, V)
+        o1p(2, 3)
+        o1p(3, 3)
+        o1p(3, 2)
+        o1p(2, 0)
+        de(5, 0, S)
+        te(5, 1, S)
+        o0(4, 3)
+        oe(4, 2, S)
+        oe(4, 3, S)
+        im(4)
+        o0(4, 1)
+        o1p(3, 0)
+        im(5)
+        o0(4, 0)
+        dh(6, 0)
+        xq(4)
+        oe(4, 1, S)
+        tr(5, 0)
+        dh(6, 1)
+        oe(4, 0, S)
+        te(5, 0, S)
+        dh(6, 2)
+        iq(5)
+        o1p(2, 1)
+        o1p(3, 1)
+        iq(4)
+        fq(5)
+        de(6, 0, S)
+        dh(6, 3)
+        de(6, 1, S)
+        lx(6)
+        de(6, 2, S)
+        tr(6, 0)
+        de(6, 3, S)
+        st(2)
+        lx(7)
+        xm(6, 256, 512, V)
+        xq(5)
+        o1p(4, 3)
+        o0(5, 1)
+        tr(6, 1)
+        te(6, 0, S)
+        o0(5, 3)
+        o1p(4, 2)
+        oe(5, 1, S)
+        te(6, 1, S)
+        o0(5, 2)
+        im(6)
+        xm(6, 0, 256, V)
+        xm(7, 0, 256, V)
+        oe(5, 3, S)
+        st(4)
+        dh(7, 3)
+        dh(7, 1)
+        oe(5, 2, S)
+        iq(6)
+        de(7, 3, S)
+        dh(7, 0)
+        st(3)
+        de(7, 1, S)
+        de(7, 0, S)
+        o1p(4, 0)
+        dh(7, 2)
+        o0(5, 0)
+        fq(6)
+        xm(7, 256, 512, V)
+        xq(6)
+        de(7, 2, S)
+        o1p(5, 3)
+        o0(6, 1)
+        im(7)
+        oe(5, 0, S)
+        o0(6, 0)
+        xq(7)
+        tr(7, 1)
+        iq(7)
+        oe(6, 0, S)
+        oe(6, 1, S)
+        o1p(4, 1)
+        o1p(5, 0)
+        o0(6, 2)
+        te(7, 1, S)
+        o1p(6, 3)
+        st(5)
+        o0(6, 3)
+        o1p(6, 0)
+        st(6, 0, 2)
+        tr(7, 0)
+        o1p(5, 2)
+        oe(6, 2, S)
+        oe(6, 3, S)
+        st(6, 2, 4)
+        o1p(6, 2)
+        o1p(7, 3)
+        o1p(7, 2)
+        o1p(5, 1)
+        o1p(6, 1)
+        o1p(7, 1)
+        o1p(7, 0)
+        te(7, 0, S)
+        pe(3, V)
+        pe(2, S)
+        fq(7)
+        pe(1, V)
+        pe(0, S)
+        o0(7, 3)
+        sp(2, 4)
+        o0(7, 2)
+        oe(7, 2, S)
+        o0(7, 1)
+        oe(7, 3, V)
+        sp(0, 2)
+        st(7, 2, 4)
+        o0(7, 0)
+        oe(7, 1, S)
+        oe(7, 0, V)
+        st(7, 0, 2)

@@ -12,596 +12,392 @@ E5M2 = mybir.dt.float8_e5m2_x4
 ALU = mybir.AluOpType
 
 P = 128
+GRAPHS = 4
 NODES = 1024
-D = 512
-TOKENS = 4096
+FEATURES = 512
+TOKENS = GRAPHS * NODES
 UNIT = 512
 UNITS = TOKENS // UNIT
+TILES = UNIT // P
+HALF = FEATURES // 2
 
-FLOPS = 2 * 4 * NODES * NODES * D + 2 * 2 * TOKENS * D * D
-BYTES = TOKENS * D * 2 + NODES * NODES * 2 + D * D * 2 + TOKENS * D * 6 + TOKENS * D * 4 + D * D * 4
+X_VECTOR_COLUMNS = 256
 
-S = "scalar"
-V = "vector"
+FLOPS = 2 * GRAPHS * NODES * NODES * FEATURES + 2 * 2 * TOKENS * FEATURES * FEATURES
+BYTES = (
+    2 * (2 * TOKENS * FEATURES + NODES * NODES + FEATURES * FEATURES)
+    + 4 * (2 * TOKENS * FEATURES + FEATURES * FEATURES)
+)
 
 
 def tile_gcn_pb_v_kernel(tc, x, ahat, gcn1_w, gcn1_b, h, grad_out, out_0, out_1):
     nc = tc.nc
-    h2 = h.rearrange("b n f -> (b n) f")
-    g2 = grad_out.rearrange("b n f -> (b n) f")
+    h_tokens = h.rearrange("b n f -> (b n) f")
+    grad_tokens = grad_out.rearrange("b n f -> (b n) f")
 
     with ExitStack() as ctx:
         keep = ctx.enter_context(tc.tile_pool(name="keep", bufs=1))
-        pool = ctx.enter_context(tc.tile_pool(name="stream", bufs=3))
+        stream = ctx.enter_context(tc.tile_pool(name="stream", bufs=2))
         psum = ctx.enter_context(tc.psum_pool(name="psum", bufs=1))
 
-        ident = keep.tile([P, P], F32, name="ident")
-        make_identity(nc, ident[:])
-        ident_bf = keep.tile([P, P], BF16, name="ident_bf")
-        make_identity(nc, ident_bf[:])
+        identity = keep.tile([P, P], F32, name="identity")
+        make_identity(nc, identity[:])
+
         ctx.enter_context(tc.manual_schedule())
 
-        a_codes = []
-        a_scales = []
+        ahat_codes = []
+        ahat_scales = []
         for s in range(2):
-            a_codes.append(keep.tile([P, NODES], U32, name="a_codes%d" % s, align_bytes=64))
-            a_scales.append(keep.tile([P, NODES], U8, name="a_scales%d" % s, align_bytes=64))
-        w_codes = keep.tile([P, D], U32, name="w_codes", align_bytes=64)
-        w_scales = keep.tile([P, D], U8, name="w_scales", align_bytes=64)
-        o1 = keep.tile([P, 4, D], F32, name="out1_rows", align_bytes=64)
-        acc = []
-        for c in range(4):
-            acc.append(psum.tile([P, D], F32, name="acc%d" % c, bufs=1))
+            ahat_codes.append(keep.tile([P, NODES], U32, name="ahat_codes%d" % s, align_bytes=64))
+            ahat_scales.append(keep.tile([P, NODES], U8, name="ahat_scales%d" % s, align_bytes=64))
+        w_codes = keep.tile([P, FEATURES], U32, name="w_codes", align_bytes=64)
+        w_scales = keep.tile([P, FEATURES], U8, name="w_scales", align_bytes=64)
 
-        ah, wt, hg, xs, zt, zc, av, qv, tok, gv, fc, xt, xc, work, ob = {}, {}, {}, {}, {}, {}, {}, {}, {}, {}, {}, {}, {}, {}, {}
-        o1view = out_1.rearrange("(d p) f -> p d f", p=P)
+        out_1_banks = []
+        for d in range(FEATURES // P):
+            out_1_banks.append(psum.tile([P, FEATURES], F32, name="out_1_bank%d" % d, bufs=1))
+        out_1_rows = keep.tile([P, FEATURES // P, FEATURES], F32, name="out_1_rows", align_bytes=64)
 
-        def new_bank():
-            return psum.tile([P, D], F32, name="work", tag="work", bufs=4)
+        h_rows, grad_rows, x_rows, ahat_rows, w_rows = {}, {}, {}, {}, {}
+        dz2_grouped, dz2_mx = {}, {}
+        dz1, dz1_grouped, dz1_token_mx, dz1_feature_mx = {}, {}, {}, {}
+        x_grouped, x_mx = {}, {}
+        turned, banks, out_0_rows = {}, {}, {}
 
-        def codes(key, bufs):
-            c = pool.tile([P, D], U32, name=key + "_codes", tag=key + "_codes", bufs=bufs, align_bytes=64)
-            s = pool.tile([P, D], U8, name=key + "_scales", tag=key + "_scales", bufs=bufs, align_bytes=64)
-            return c, s
-
-        def rows(k):
+        def unit_rows(k):
             return slice(UNIT * k, UNIT * (k + 1))
 
-        def copy(engine, out, in_):
-            if engine == S:
-                nc.scalar.copy(out=out, in_=in_)
-            else:
-                nc.vector.tensor_copy(out=out, in_=in_)
+        def work_bank():
+            return psum.tile([P, FEATURES], F32, name="work_bank", tag="work_bank", bufs=4)
 
-        def la(half, pair):
-            if half not in ah:
-                ah[half] = pool.tile([P, 4, NODES], BF16, name="ahat_rows", tag="ahat_rows", bufs=2, align_bytes=64)
-            view = ahat[rows(half), :].rearrange("(m t) j -> m t j", t=4)
-            nc.sync.dma_start(out=ah[half][:, 2 * pair:2 * pair + 2, :], in_=view[:, 2 * pair:2 * pair + 2, :])
+        def codes_and_scales(name, bufs):
+            codes = stream.tile([P, UNIT], U32, name=name + "_codes", tag=name + "_codes", bufs=bufs, align_bytes=64)
+            scales = stream.tile([P, UNIT], U8, name=name + "_scales", tag=name + "_scales", bufs=bufs, align_bytes=64)
+            return codes, scales
 
-        def lw():
-            wt[0] = pool.tile([P, 4, D], BF16, name="w_rows", tag="w_rows", bufs=1, align_bytes=64)
-            nc.sync.dma_start(out=wt[0][:], in_=gcn1_w.rearrange("(d p) f -> p d f", p=P))
 
-        def lg(k, c0=0, c1=D):
-            if ("g", k) not in hg:
-                hg["g", k] = pool.tile([P, 4, D], BF16, name="g_rows", tag="g_rows", bufs=4, align_bytes=64)
-            nc.sync.dma_start(out=hg["g", k][:, :, c0:c1], in_=g2[rows(k), c0:c1].rearrange("(p j) f -> p j f", j=4))
+        def load_grad(k, c0=0, c1=FEATURES):
+            if k not in grad_rows:
+                grad_rows[k] = stream.tile([P, 4, FEATURES], BF16, name="grad_rows", tag="grad_rows", bufs=4, align_bytes=64)
+            view = grad_tokens[unit_rows(k), c0:c1].rearrange("(p j) f -> p j f", j=4)
+            nc.sync.dma_start(out=grad_rows[k][:, :, c0:c1], in_=view)
 
-        def lh(k, c0=0, c1=D):
-            if ("h", k) not in hg:
-                hg["h", k] = pool.tile([P, 4, D], F32, name="h_rows", tag="h_rows", bufs=4, align_bytes=64)
-            nc.sync.dma_start(out=hg["h", k][:, :, c0:c1], in_=h2[rows(k), c0:c1].rearrange("(p j) f -> p j f", j=4))
+        def load_h(k, c0=0, c1=FEATURES):
+            if k not in h_rows:
+                h_rows[k] = stream.tile([P, 4, FEATURES], F32, name="h_rows", tag="h_rows", bufs=4, align_bytes=64)
+            view = h_tokens[unit_rows(k), c0:c1].rearrange("(p j) f -> p j f", j=4)
+            nc.sync.dma_start(out=h_rows[k][:, :, c0:c1], in_=view)
 
-        def lx(k):
-            xs[k] = pool.tile([P, 4, D], BF16, name="x_rows", tag="x_rows", bufs=3, align_bytes=64)
-            nc.sync.dma_start(out=xs[k][:], in_=x[rows(k), :].rearrange("(p j) w -> p j w", j=4))
+        def load_x(k):
+            x_rows[k] = stream.tile([P, 4, FEATURES], BF16, name="x_rows", tag="x_rows", bufs=4, align_bytes=64)
+            nc.sync.dma_start(out=x_rows[k][:], in_=x[unit_rows(k), :].rearrange("(p j) w -> p j w", j=4))
 
-        def every_second(key, rows_tile, first, pair):
-            bank = new_bank()
+        def load_ahat(half):
+            ahat_rows[half] = stream.tile([P, 4, NODES], BF16, name="ahat_rows", tag="ahat_rows", bufs=2, align_bytes=64)
+            view = ahat[unit_rows(half), :].rearrange("(m t) j -> m t j", t=4)
+            for pair in range(2):
+                rows = slice(2 * pair, 2 * pair + 2)
+                nc.sync.dma_start(out=ahat_rows[half][:, rows, :], in_=view[:, rows, :])
+
+        def load_w():
+            w_rows[0] = stream.tile([P, 4, FEATURES], BF16, name="w_rows", tag="w_rows", bufs=1, align_bytes=64)
+            nc.sync.dma_start(out=w_rows[0][:], in_=gcn1_w.rearrange("(d p) f -> p d f", p=P))
+
+
+        def transpose_two_tiles(key, tiles, pairs_of):
+            bank = work_bank()
             for i in range(2):
-                words = rows_tile[:, 2 * pair + i, :].bitcast(F32)
+                pairs = tiles[i].bitcast(F32)
                 for u in range(2):
-                    c0 = 256 * i + 128 * u
-                    nc.tensor.transpose(bank[:, c0:c0 + P], words[:, first + u:first + 256:2], ident[:])
-            work[key] = bank
+                    c0 = P * (2 * i + u)
+                    nc.tensor.transpose(bank[:, c0 : c0 + P], pairs[:, pairs_of(u)], identity[:])
+            banks[key] = bank
 
-        def turned_out(key, gkey, pair, engine):
-            if gkey not in gv:
-                gv[gkey] = pool.tile([P, 4 * D], BF16, name="grouped", tag="grouped", bufs=4, align_bytes=64)
-            out = gv[gkey][:, 1024 * pair:1024 * (pair + 1)].bitcast(F32).rearrange("q (t r u) -> q t r u", t=2, u=2)
-            copy(engine, out, work[key][:].rearrange("q (t u r) -> q t r u", t=2, u=2))
+        def copy_transposed(key, name, pair):
+            if name not in turned:
+                turned[name] = stream.tile([P, UNIT, 4], BF16, name="turned", tag="turned", bufs=4, align_bytes=64)
+            rows = turned[name][:, 2 * P * pair : 2 * P * (pair + 1), :].rearrange("q r v -> q (r v)")
+            nc.scalar.copy(
+                out=rows.bitcast(F32).rearrange("q (t r u) -> q t r u", t=2, u=2),
+                in_=banks[key][:].rearrange("q (t u r) -> q t r u", t=2, u=2),
+            )
 
-        def at(half, s, pair):
-            every_second(("a", half, s, pair), ah[half], 256 * s, pair)
+        def every_second_pair(first):
+            return lambda u: slice(first + u, first + HALF, 2)
 
-        def ae(half, s, pair, engine):
-            turned_out(("a", half, s, pair), ("a", half, s), pair, engine)
+        def side_by_side(u):
+            return slice(P * u, P * (u + 1))
 
-        def aq(half, s, pair):
-            cols = slice(UNIT * half + 256 * pair, UNIT * half + 256 * (pair + 1))
-            src = gv["a", half, s][:, 1024 * pair:1024 * (pair + 1)]
-            nc.vector.quantize_mx(out=a_codes[s][:, cols].bitcast(E4M3), scales=a_scales[s][:, cols], in_=src)
 
-        def wtr(pair):
-            every_second(("w", pair), wt[0], 0, pair)
+        def transpose_ahat(half, pair):
+            tiles = [ahat_rows[half][:, 2 * pair + i, :] for i in range(2)]
+            for s in range(2):
+                transpose_two_tiles(("ahat", half, s, pair), tiles, every_second_pair(HALF * s))
+                copy_transposed(("ahat", half, s, pair), ("ahat", half, s), pair)
 
-        def we(pair, engine):
-            turned_out(("w", pair), "w", pair, engine)
+        def quantize_ahat(half, pair):
+            cols = slice(UNIT * half + 2 * P * pair, UNIT * half + 2 * P * (pair + 1))
+            for s in range(2):
+                values = turned["ahat", half, s][:, 2 * P * pair : 2 * P * (pair + 1), :]
+                nc.vector.quantize_mx(
+                    out=ahat_codes[s][:, cols].bitcast(E4M3),
+                    scales=ahat_scales[s][:, cols],
+                    in_=values.rearrange("q r v -> q (r v)"),
+                )
 
-        def wq():
-            nc.vector.quantize_mx(out=w_codes[:].bitcast(E4M3), scales=w_scales[:], in_=gv["w"][:])
+        def transpose_w():
+            for pair in range(2):
+                tiles = [w_rows[0][:, 2 * pair + i, :] for i in range(2)]
+                transpose_two_tiles(("w", pair), tiles, every_second_pair(0))
+                copy_transposed(("w", pair), "w", pair)
 
-        def z(k, f0=0, f1=D):
-            if k not in zt:
-                zt[k] = pool.tile([P, D, 4], BF16, name="dz2", tag="dz2", bufs=3, align_bytes=64)
+        def quantize_w():
+            nc.vector.quantize_mx(
+                out=w_codes[:].bitcast(E4M3), scales=w_scales[:], in_=turned["w"][:].rearrange("q r v -> q (r v)")
+            )
+
+
+        def make_dz2(k, c0=0, c1=FEATURES):
+            if k not in dz2_grouped:
+                dz2_grouped[k] = stream.tile([P, FEATURES, 4], BF16, name="dz2_grouped", tag="dz2_grouped", bufs=3, align_bytes=64)
             nc.vector.scalar_tensor_tensor(
-                out=zt[k][:, f0:f1, :],
-                in0=hg["h", k][:, :, f0:f1].rearrange("p j f -> p f j"),
+                out=dz2_grouped[k][:, c0:c1, :],
+                in0=h_rows[k][:, :, c0:c1].rearrange("p j f -> p f j"),
                 scalar=0.0,
-                in1=hg["g", k][:, :, f0:f1].rearrange("p j f -> p f j"),
+                in1=grad_rows[k][:, :, c0:c1].rearrange("p j f -> p f j"),
                 op0=ALU.is_gt,
                 op1=ALU.mult,
             )
 
-        def zq(k, f0=0, f1=D):
-            if k not in zc:
-                zc[k] = codes("dz2", 4)
-            c, s = zc[k]
-            nc.vector.quantize_mx(out=c[:, f0:f1].bitcast(E5M2), scales=s[:, f0:f1], in_=zt[k][:, f0:f1, :].rearrange("p f j -> p (f j)"))
+        def quantize_dz2(k):
+            dz2_mx[k] = codes_and_scales("dz2", 4)
+            codes, scales = dz2_mx[k]
+            nc.vector.quantize_mx(
+                out=codes[:].bitcast(E5M2), scales=scales[:], in_=dz2_grouped[k][:].rearrange("p f j -> p (f j)")
+            )
 
-        def dh(k, t):
+
+        def multiply_dz1(k):
             half = k % 2
-            work["d", k, t] = new_bank()
-            cols = slice(UNIT * half + P * t, UNIT * half + P * (t + 1))
-            for s in range(2):
-                c, sc = zc[k - half + s]
-                nc.tensor.matmul_mx(
-                    out=work["d", k, t][:],
-                    lhsT=a_codes[s][:, cols].bitcast(E4M3), lhsT_scale=a_scales[s][:, cols],
-                    rhs=c[:].bitcast(E5M2), rhs_scale=sc[:],
-                    start=(s == 0), stop=(s == 1),
+            for t in range(TILES):
+                cols = slice(UNIT * half + P * t, UNIT * half + P * (t + 1))
+                banks["dz1", k, t] = work_bank()
+                for s in range(2):
+                    codes, scales = dz2_mx[k - half + s]
+                    nc.tensor.matmul_mx(
+                        out=banks["dz1", k, t][:],
+                        lhsT=ahat_codes[s][:, cols].bitcast(E4M3),
+                        lhsT_scale=ahat_scales[s][:, cols],
+                        rhs=codes[:].bitcast(E5M2),
+                        rhs_scale=scales[:],
+                        start=(s == 0),
+                        stop=(s == 1),
+                    )
+
+        def copy_dz1(k):
+            dz1[k] = stream.tile([P, TILES, FEATURES], BF16, name="dz1", tag="dz1", bufs=3, align_bytes=64)
+            for t in range(TILES):
+                nc.scalar.copy(
+                    out=dz1[k][:, t, :].rearrange("p (u q e) -> p u q e", u=2, e=2),
+                    in_=banks["dz1", k, t][:].rearrange("p (q u e) -> p u q e", u=2, e=2),
                 )
 
-        def de(k, t, engine):
-            if k not in av:
-                av[k] = pool.tile([P, 4, D], BF16, name="dz1", tag="dz1", bufs=3, align_bytes=64)
-            copy(engine, av[k][:, t, :].rearrange("p (u q e) -> p u q e", u=2, e=2),
-                 work["d", k, t][:].rearrange("p (q u e) -> p u q e", u=2, e=2))
 
-        def im(k):
-            qv[k] = pool.tile([P, D, 4], BF16, name="dz1_tok", tag="dz1_tok", bufs=2, align_bytes=64)
+        def group_dz1_tokens(k):
+            dz1_grouped[k] = stream.tile([P, FEATURES, TILES], BF16, name="dz1_grouped", tag="dz1_grouped", bufs=2, align_bytes=64)
             nc.vector.tensor_copy(
-                out=qv[k][:].rearrange("p (c i) t -> p c t i", i=4),
-                in_=av[k][:].rearrange("p t (c i) -> p c t i", i=4),
+                out=dz1_grouped[k][:].rearrange("p (c i) t -> p c t i", i=4),
+                in_=dz1[k][:].rearrange("p t (c i) -> p c t i", i=4),
             )
 
-        def iq(k):
-            tok[k] = codes("tok", 4)
-            c, s = tok[k]
-            nc.vector.quantize_mx(out=c[:].bitcast(E5M2), scales=s[:], in_=qv[k][:].rearrange("p f t -> p (f t)"))
-
-        def tr(k, pair):
-            bank = new_bank()
-            for i in range(2):
-                words = av[k][:, 2 * pair + i, :].bitcast(F32)
-                for u in range(2):
-                    c0 = 256 * i + 128 * u
-                    nc.tensor.transpose(bank[:, c0:c0 + P], words[:, 128 * u:128 * (u + 1)], ident[:])
-            work["t", k, pair] = bank
-
-        def te(k, pair, engine):
-            turned_out(("t", k, pair), ("t", k), pair, engine)
-
-        def fq(k):
-            fc[k] = codes("feat", 2)
-            c, s = fc[k]
-            nc.vector.quantize_mx(out=c[:].bitcast(E5M2), scales=s[:], in_=gv["t", k][:])
-
-        def o0(k, t):
-            bank = new_bank()
-            work["o", k, t] = bank
-            c, s = fc[k]
-            cols = slice(P * t, P * (t + 1))
-            nc.tensor.matmul_mx(
-                out=bank[:], lhsT=c[:, cols].bitcast(E5M2), lhsT_scale=s[:, cols],
-                rhs=w_codes[:].bitcast(E4M3), rhs_scale=w_scales[:], start=True, stop=True,
+        def quantize_dz1_tokens(k):
+            dz1_token_mx[k] = codes_and_scales("dz1_token", 4)
+            codes, scales = dz1_token_mx[k]
+            nc.vector.quantize_mx(
+                out=codes[:].bitcast(E5M2), scales=scales[:], in_=dz1_grouped[k][:].rearrange("p f t -> p (f t)")
             )
 
-        def oe(k, t, engine):
-            if k not in ob:
-                ob[k] = pool.tile([P, 4, D], F32, name="out_rows", tag="out_rows", bufs=3, align_bytes=64)
-            copy(engine, ob[k][:, t, :], work["o", k, t][:])
+        def transpose_dz1(k):
+            for pair in range(2):
+                tiles = [dz1[k][:, 2 * pair + i, :] for i in range(2)]
+                transpose_two_tiles(("dz1T", k, pair), tiles, side_by_side)
+            for pair in range(2):
+                copy_transposed(("dz1T", k, pair), ("dz1T", k), pair)
 
-        def st(k, t0=0, t1=4):
-            view = out_0[rows(k), :].rearrange("(p t) w -> p t w", t=4)
-            nc.sync.dma_start(out=view[:, t0:t1, :], in_=ob[k][:, t0:t1, :])
+        def quantize_dz1_features(k):
+            dz1_feature_mx[k] = codes_and_scales("dz1_feature", 2)
+            codes, scales = dz1_feature_mx[k]
+            nc.vector.quantize_mx(
+                out=codes[:].bitcast(E5M2), scales=scales[:], in_=turned["dz1T", k][:].rearrange("q r v -> q (r v)")
+            )
 
-        def xp(k, half):
-            bank = psum.tile([P, 2 * D], BF16, name="xbank", tag="work", bufs=4)
-            for q in range(2):
-                cols = slice(256 * half + 128 * q, 256 * half + 128 * (q + 1))
-                nc.tensor.matmul(
-                    out=bank[:, 512 * q:512 * (q + 1)],
-                    lhsT=ident_bf[:],
-                    rhs=xs[k][:, :, cols].rearrange("p j w -> p w j"),
-                    start=True, stop=True,
+
+        def multiply_out_0(k):
+            codes, scales = dz1_feature_mx[k]
+            for t in range(TILES):
+                cols = slice(P * t, P * (t + 1))
+                banks["out_0", k, t] = work_bank()
+                nc.tensor.matmul_mx(
+                    out=banks["out_0", k, t][:],
+                    lhsT=codes[:, cols].bitcast(E5M2),
+                    lhsT_scale=scales[:, cols],
+                    rhs=w_codes[:].bitcast(E4M3),
+                    rhs_scale=w_scales[:],
+                    start=True,
+                    stop=True,
                 )
-            work["x", k, half] = bank
 
-        def new_xt(k):
-            if k not in xt:
-                xt[k] = pool.tile([P, D, 4], BF16, name="x_grouped", tag="x_grouped", bufs=2, align_bytes=64)
-            return xt[k]
+        def store_out_0(k, pieces):
+            out_0_rows[k] = stream.tile([P, TILES, FEATURES], F32, name="out_0_rows", tag="out_0_rows", bufs=3, align_bytes=64)
+            view = out_0[unit_rows(k), :].rearrange("(p t) w -> p t w", t=TILES)
+            step = TILES // pieces
+            for t in range(TILES):
+                nc.scalar.copy(out=out_0_rows[k][:, t, :], in_=banks["out_0", k, t][:])
+                if (t + 1) % step == 0:
+                    done = slice(t + 1 - step, t + 1)
+                    nc.sync.dma_start(out=view[:, done, :], in_=out_0_rows[k][:, done, :])
 
-        def xe(k, half, engine):
-            out = new_xt(k)[:, 256 * half:256 * (half + 1), :].rearrange("p w j -> p (w j)")
-            copy(engine, out, work["x", k, half][:])
 
-        def xm(k, c0, c1, engine):
-            copy(engine, new_xt(k)[:, c0:c1, :].rearrange("p (c i) j -> p c j i", i=4),
-                 xs[k][:, :, c0:c1].rearrange("p j (c i) -> p c j i", i=4))
-
-        def xq(k):
-            xc[k] = codes("x", 4)
-            c, s = xc[k]
-            nc.vector.quantize_mx(out=c[:].bitcast(E4M3), scales=s[:], in_=xt[k][:].rearrange("p w j -> p (w j)"))
-
-        def o1p(k, d):
-            xcod, xsc = xc[k]
-            tcod, tsc = tok[k]
-            cols = slice(P * d, P * (d + 1))
-            nc.tensor.matmul_mx(
-                out=acc[d][:], lhsT=xcod[:, cols].bitcast(E4M3), lhsT_scale=xsc[:, cols],
-                rhs=tcod[:].bitcast(E5M2), rhs_scale=tsc[:], start=(k == 0), stop=(k == UNITS - 1),
+        def group_x(k, c0, c1, copy):
+            if k not in x_grouped:
+                x_grouped[k] = stream.tile([P, FEATURES, 4], BF16, name="x_grouped", tag="x_grouped", bufs=2, align_bytes=64)
+            copy(
+                out=x_grouped[k][:, c0:c1, :].rearrange("p (c i) j -> p c j i", i=4),
+                in_=x_rows[k][:, :, c0:c1].rearrange("p j (c i) -> p c j i", i=4),
             )
 
-        def pe(d, engine):
-            copy(engine, o1[:, d, :].rearrange("p (q u e) -> p q u e", u=2, e=2),
-                 acc[d][:].rearrange("p (u q e) -> p q u e", u=2, e=2))
+        def quantize_x(k):
+            x_mx[k] = codes_and_scales("x", 4)
+            codes, scales = x_mx[k]
+            nc.vector.quantize_mx(
+                out=codes[:].bitcast(E4M3), scales=scales[:], in_=x_grouped[k][:].rearrange("p w j -> p (w j)")
+            )
 
-        def sp(d0, d1):
-            nc.sync.dma_start(out=o1view[:, d0:d1, :], in_=o1[:, d0:d1, :])
+        def multiply_out_1(k):
+            x_codes, x_scales = x_mx[k]
+            codes, scales = dz1_token_mx[k]
+            for d in range(FEATURES // P):
+                cols = slice(P * d, P * (d + 1))
+                nc.tensor.matmul_mx(
+                    out=out_1_banks[d][:],
+                    lhsT=x_codes[:, cols].bitcast(E4M3),
+                    lhsT_scale=x_scales[:, cols],
+                    rhs=codes[:].bitcast(E5M2),
+                    rhs_scale=scales[:],
+                    start=(k == 0),
+                    stop=(k == UNITS - 1),
+                )
 
-        lg(0, 256, 512)
-        lh(0, 256, 512)
-        la(0, 0)
-        lg(0, 0, 256)
-        lh(0, 0, 256)
-        z(0, 256, 512)
-        lh(1, 0, 256)
-        z(0, 0, 256)
-        at(0, 1, 0)
-        at(0, 0, 0)
-        ae(0, 1, 0, S)
-        lg(1)
-        zq(0)
-        la(0, 1)
-        lh(1, 256, 512)
-        z(1, 0, 256)
-        zq(1, 0, 256)
-        at(0, 1, 1)
-        ae(0, 1, 1, S)
-        at(0, 0, 1)
-        lg(2)
-        ae(0, 0, 0, S)
-        lh(2)
-        ae(0, 0, 1, S)
-        z(1, 256, 512)
-        aq(0, 0, 0)
-        zq(1, 256, 512)
-        aq(0, 1, 0)
-        aq(0, 0, 1)
-        la(1, 0)
-        dh(0, 1)
-        aq(0, 1, 1)
-        la(1, 1)
-        de(0, 1, S)
-        dh(0, 3)
-        de(0, 3, S)
-        z(2, 0, 256)
-        dh(0, 0)
-        dh(0, 2)
-        de(0, 0, S)
-        lw()
-        z(2, 256, 512)
-        at(1, 0, 0)
-        at(1, 1, 1)
-        tr(0, 0)
-        de(0, 2, S)
-        lh(3)
-        ae(1, 0, 0, S)
-        at(1, 0, 1)
-        tr(0, 1)
-        im(0)
-        ae(1, 1, 1, S)
-        te(0, 0, S)
-        at(1, 1, 0)
-        aq(1, 1, 1)
-        wtr(0)
-        ae(1, 0, 1, S)
-        iq(0)
-        zq(2)
-        ae(1, 1, 0, S)
-        te(0, 1, S)
-        aq(1, 0, 0)
-        aq(1, 1, 0)
-        wtr(1)
-        we(1, S)
-        lx(0)
-        aq(1, 0, 1)
-        we(0, S)
-        dh(1, 1)
-        xm(0, 256, 512, S)
-        fq(0)
-        dh(1, 0)
-        xm(0, 0, 256, V)
-        de(1, 1, S)
-        wq()
-        dh(1, 3)
-        de(1, 0, S)
-        lg(3)
-        o0(0, 3)
-        lx(1)
-        de(1, 3, S)
-        z(3, 256, 512)
-        o0(0, 2)
-        oe(0, 3, S)
-        lg(4)
-        dh(1, 2)
-        de(1, 2, S)
-        z(3, 0, 256)
-        xm(1, 256, 512, V)
-        lx(2)
-        o0(0, 0)
-        oe(0, 2, S)
-        zq(3)
-        tr(1, 1)
-        tr(1, 0)
-        oe(0, 0, S)
-        te(1, 1, S)
-        xm(1, 0, 256, V)
-        im(1)
-        o0(0, 1)
-        dh(2, 0)
-        te(1, 0, S)
-        fq(1)
-        lh(5)
-        xq(0)
-        lg(5)
-        dh(2, 2)
-        lg(7)
-        oe(0, 1, S)
-        dh(2, 3)
-        lh(4)
-        dh(2, 1)
-        de(2, 0, S)
-        de(2, 2, S)
-        de(2, 3, S)
-        de(2, 1, S)
-        lx(3)
-        z(5, 0, 256)
-        o0(1, 0)
-        iq(1)
-        lh(7)
-        o0(1, 3)
-        oe(1, 0, S)
-        o0(1, 1)
-        tr(2, 0)
-        dh(3, 0)
-        xq(1)
-        lx(4)
-        z(5, 256, 512)
-        xm(2, 0, 256, S)
-        o1p(0, 3)
-        oe(1, 3, S)
-        o1p(0, 0)
-        lg(6)
-        o1p(1, 3)
-        z(4, 256, 512)
-        o0(1, 2)
-        oe(1, 1, S)
-        te(2, 0, S)
-        dh(3, 1)
-        z(4, 0, 256)
-        de(3, 0, S)
-        lh(6)
-        o1p(0, 1)
-        im(2)
-        tr(2, 1)
-        oe(1, 2, S)
-        o1p(0, 2)
-        dh(3, 3)
-        de(3, 1, S)
-        te(2, 1, S)
-        dh(3, 2)
-        fq(2)
-        de(3, 3, S)
-        zq(4)
-        de(3, 2, S)
-        o1p(1, 0)
-        tr(3, 1)
-        o0(2, 3)
-        xm(3, 256, 512, S)
-        zq(5)
-        te(3, 1, S)
-        tr(3, 0)
-        xm(2, 256, 512, S)
-        z(6, 0, 256)
-        o0(2, 0)
-        te(3, 0, S)
-        st(0)
-        oe(2, 3, S)
-        oe(2, 0, S)
-        o0(2, 1)
-        dh(4, 1)
-        xq(2)
-        fq(3)
-        oe(2, 1, S)
-        o0(2, 2)
-        dh(4, 0)
-        de(4, 1, S)
-        o0(3, 3)
-        oe(2, 2, S)
-        oe(3, 3, S)
-        o0(3, 1)
-        im(3)
-        xm(3, 0, 256, V)
-        de(4, 0, S)
-        oe(3, 1, S)
-        o1p(1, 1)
-        iq(2)
-        dh(4, 2)
-        o1p(1, 2)
-        z(6, 256, 512)
-        o0(3, 0)
-        oe(3, 0, S)
-        dh(4, 3)
-        z(7, 256, 512)
-        tr(4, 0)
-        de(4, 2, S)
-        de(4, 3, S)
-        z(7, 0, 256)
-        te(4, 0, S)
-        lx(5)
-        st(1)
-        zq(6)
-        tr(4, 1)
-        xq(3)
-        te(4, 1, S)
-        o0(3, 2)
-        xm(4, 256, 512, S)
-        dh(5, 3)
-        dh(5, 2)
-        fq(4)
-        iq(3)
-        o1p(2, 2)
-        de(5, 3, S)
-        zq(7)
-        dh(5, 1)
-        xm(5, 0, 256, V)
-        oe(3, 2, S)
-        de(5, 2, S)
-        de(5, 1, S)
-        xm(5, 256, 512, S)
-        dh(5, 0)
-        tr(5, 1)
-        o0(4, 2)
-        xm(4, 0, 256, V)
-        o1p(2, 3)
-        o1p(3, 3)
-        o1p(3, 2)
-        o1p(2, 0)
-        de(5, 0, S)
-        te(5, 1, S)
-        o0(4, 3)
-        oe(4, 2, S)
-        oe(4, 3, S)
-        im(4)
-        o0(4, 1)
-        o1p(3, 0)
-        im(5)
-        o0(4, 0)
-        dh(6, 0)
-        xq(4)
-        oe(4, 1, S)
-        tr(5, 0)
-        dh(6, 1)
-        oe(4, 0, S)
-        te(5, 0, S)
-        dh(6, 2)
-        iq(5)
-        o1p(2, 1)
-        o1p(3, 1)
-        iq(4)
-        fq(5)
-        de(6, 0, S)
-        dh(6, 3)
-        de(6, 1, S)
-        lx(6)
-        de(6, 2, S)
-        tr(6, 0)
-        de(6, 3, S)
-        st(2)
-        lx(7)
-        xm(6, 256, 512, V)
-        xq(5)
-        o1p(4, 3)
-        o0(5, 1)
-        tr(6, 1)
-        te(6, 0, S)
-        o0(5, 3)
-        o1p(4, 2)
-        oe(5, 1, S)
-        te(6, 1, S)
-        o0(5, 2)
-        im(6)
-        xm(6, 0, 256, V)
-        xm(7, 0, 256, V)
-        oe(5, 3, S)
-        st(4)
-        dh(7, 3)
-        dh(7, 1)
-        oe(5, 2, S)
-        iq(6)
-        de(7, 3, S)
-        dh(7, 0)
-        st(3)
-        de(7, 1, S)
-        de(7, 0, S)
-        o1p(4, 0)
-        dh(7, 2)
-        o0(5, 0)
-        fq(6)
-        xm(7, 256, 512, V)
-        xq(6)
-        de(7, 2, S)
-        o1p(5, 3)
-        o0(6, 1)
-        im(7)
-        oe(5, 0, S)
-        o0(6, 0)
-        xq(7)
-        tr(7, 1)
-        iq(7)
-        oe(6, 0, S)
-        oe(6, 1, S)
-        o1p(4, 1)
-        o1p(5, 0)
-        o0(6, 2)
-        te(7, 1, S)
-        o1p(6, 3)
-        st(5)
-        o0(6, 3)
-        o1p(6, 0)
-        st(6, 0, 2)
-        tr(7, 0)
-        o1p(5, 2)
-        oe(6, 2, S)
-        oe(6, 3, S)
-        st(6, 2, 4)
-        o1p(6, 2)
-        o1p(7, 3)
-        o1p(7, 2)
-        o1p(5, 1)
-        o1p(6, 1)
-        o1p(7, 1)
-        o1p(7, 0)
-        te(7, 0, S)
-        pe(3, V)
-        pe(2, S)
-        fq(7)
-        pe(1, V)
-        pe(0, S)
-        o0(7, 3)
-        sp(2, 4)
-        o0(7, 2)
-        oe(7, 2, S)
-        o0(7, 1)
-        oe(7, 3, V)
-        sp(0, 2)
-        st(7, 2, 4)
-        o0(7, 0)
-        oe(7, 1, S)
-        oe(7, 0, V)
-        st(7, 0, 2)
+        def store_out_1():
+            view = out_1.rearrange("(d p) f -> p d f", p=P)
+            stores = {1: slice(0, 2), 2: slice(2, 3), 3: slice(3, 4)}
+            for d in range(FEATURES // P):
+                copy = nc.scalar.copy if d % 2 == 0 else nc.vector.tensor_copy
+                copy(
+                    out=out_1_rows[:, d, :].rearrange("p (q u e) -> p q u e", u=2, e=2),
+                    in_=out_1_banks[d][:].rearrange("p (u q e) -> p q u e", u=2, e=2),
+                )
+                if d in stores:
+                    nc.sync.dma_start(out=view[:, stores[d], :], in_=out_1_rows[:, stores[d], :])
+
+
+        for c0 in range(0, FEATURES, HALF):
+            load_grad(0, c0, c0 + HALF)
+            load_h(0, c0, c0 + HALF)
+        load_grad(1)
+        load_h(1, 0, HALF)
+        load_h(1, HALF, FEATURES)
+        load_ahat(0)
+        load_grad(2)
+        load_h(2)
+        load_ahat(1)
+        load_w()
+        load_x(0)
+        load_grad(3)
+        load_h(3)
+        for k in range(1, 4):
+            load_x(k)
+
+        make_dz2(0, 0, HALF)
+        make_dz2(0, HALF, FEATURES)
+        load_grad(4)
+        load_h(4)
+        make_dz2(1, 0, HALF)
+        quantize_dz2(0)
+        make_dz2(1, HALF, FEATURES)
+        load_grad(5)
+        load_h(5)
+        transpose_ahat(0, 0)
+        transpose_ahat(0, 1)
+        quantize_dz2(1)
+        quantize_ahat(0, 0)
+        quantize_ahat(0, 1)
+
+
+        for k in range(UNITS - 2):
+            multiply_dz1(k)
+            copy_dz1(k)
+            if k > 0:
+                quantize_dz1_features(k - 1)
+            make_dz2(k + 2)
+            if k + 6 < UNITS:
+                load_grad(k + 6)
+                load_h(k + 6)
+            if k == 0:
+                transpose_dz1(k)
+                transpose_ahat(1, 0)
+                transpose_ahat(1, 1)
+                transpose_w()
+            else:
+                group_x(k - 1, X_VECTOR_COLUMNS, FEATURES, nc.scalar.copy)
+                multiply_out_0(k - 1)
+                store_out_0(k - 1, 1)
+                if k > 1:
+                    multiply_out_1(k - 2)
+                transpose_dz1(k)
+            group_dz1_tokens(k)
+            if k == 0:
+                quantize_ahat(1, 0)
+            quantize_dz2(k + 2)
+            if k > 0:
+                group_x(k - 1, 0, X_VECTOR_COLUMNS, nc.vector.tensor_copy)
+            quantize_dz1_tokens(k)
+            if k == 0:
+                quantize_ahat(1, 1)
+                quantize_w()
+            else:
+                quantize_x(k - 1)
+                if k + 3 < UNITS:
+                    load_x(k + 3)
+
+
+        multiply_dz1(6)
+        copy_dz1(6)
+        quantize_dz1_features(5)
+        group_x(5, 0, FEATURES, nc.vector.tensor_copy)
+        multiply_out_1(4)
+        multiply_out_0(5)
+        store_out_0(5, 1)
+        transpose_dz1(6)
+        group_dz1_tokens(6)
+        group_x(6, 0, FEATURES, nc.vector.tensor_copy)
+        multiply_dz1(7)
+        copy_dz1(7)
+        quantize_dz1_tokens(6)
+        quantize_dz1_features(6)
+        quantize_x(5)
+        transpose_dz1(7)
+        group_dz1_tokens(7)
+        multiply_out_0(6)
+        store_out_0(6, 2)
+        multiply_out_1(5)
+        quantize_dz1_features(7)
+        quantize_x(6)
+        group_x(7, 0, FEATURES, nc.vector.tensor_copy)
+        multiply_out_0(7)
+        store_out_0(7, 2)
+        quantize_dz1_tokens(7)
+        multiply_out_1(6)
+        quantize_x(7)
+        multiply_out_1(7)
+        store_out_1()

from contextlib import ExitStack

import concourse.mybir as mybir
from concourse.masks import make_identity

F32 = mybir.dt.float32
BF16 = mybir.dt.bfloat16
U32 = mybir.dt.uint32
U8 = mybir.dt.uint8
E4M3 = mybir.dt.float8_e4m3fn_x4
E5M2 = mybir.dt.float8_e5m2_x4
ALU = mybir.AluOpType

P = 128
GRAPHS = 4
NODES = 1024
FEATURES = 512
TOKENS = GRAPHS * NODES
UNIT = 512
UNITS = TOKENS // UNIT
TILES = UNIT // P
HALF = FEATURES // 2

X_VECTOR_COLUMNS = 256

FLOPS = 2 * GRAPHS * NODES * NODES * FEATURES + 2 * 2 * TOKENS * FEATURES * FEATURES
BYTES = (
    2 * (2 * TOKENS * FEATURES + NODES * NODES + FEATURES * FEATURES)
    + 4 * (2 * TOKENS * FEATURES + FEATURES * FEATURES)
)


def tile_gcn_pb_v_kernel(tc, x, ahat, gcn1_w, gcn1_b, h, grad_out, out_0, out_1):
    nc = tc.nc
    h_tokens = h.rearrange("b n f -> (b n) f")
    grad_tokens = grad_out.rearrange("b n f -> (b n) f")

    with ExitStack() as ctx:
        keep = ctx.enter_context(tc.tile_pool(name="keep", bufs=1))
        stream = ctx.enter_context(tc.tile_pool(name="stream", bufs=2))
        psum = ctx.enter_context(tc.psum_pool(name="psum", bufs=1))

        identity = keep.tile([P, P], F32, name="identity")
        make_identity(nc, identity[:])

        ctx.enter_context(tc.manual_schedule())

        ahat_codes = []
        ahat_scales = []
        for s in range(2):
            ahat_codes.append(keep.tile([P, NODES], U32, name="ahat_codes%d" % s, align_bytes=64))
            ahat_scales.append(keep.tile([P, NODES], U8, name="ahat_scales%d" % s, align_bytes=64))
        w_codes = keep.tile([P, FEATURES], U32, name="w_codes", align_bytes=64)
        w_scales = keep.tile([P, FEATURES], U8, name="w_scales", align_bytes=64)

        out_1_banks = []
        for d in range(FEATURES // P):
            out_1_banks.append(psum.tile([P, FEATURES], F32, name="out_1_bank%d" % d, bufs=1))
        out_1_rows = keep.tile([P, FEATURES // P, FEATURES], F32, name="out_1_rows", align_bytes=64)

        h_rows, grad_rows, x_rows, ahat_rows, w_rows = {}, {}, {}, {}, {}
        dz2_grouped, dz2_mx = {}, {}
        dz1, dz1_grouped, dz1_token_mx, dz1_feature_mx = {}, {}, {}, {}
        x_grouped, x_mx = {}, {}
        turned, banks, out_0_rows = {}, {}, {}

        def unit_rows(k):
            return slice(UNIT * k, UNIT * (k + 1))

        def work_bank():
            return psum.tile([P, FEATURES], F32, name="work_bank", tag="work_bank", bufs=4)

        def codes_and_scales(name, bufs):
            codes = stream.tile([P, UNIT], U32, name=name + "_codes", tag=name + "_codes", bufs=bufs, align_bytes=64)
            scales = stream.tile([P, UNIT], U8, name=name + "_scales", tag=name + "_scales", bufs=bufs, align_bytes=64)
            return codes, scales


        def load_grad(k, c0=0, c1=FEATURES):
            if k not in grad_rows:
                grad_rows[k] = stream.tile([P, 4, FEATURES], BF16, name="grad_rows", tag="grad_rows", bufs=4, align_bytes=64)
            view = grad_tokens[unit_rows(k), c0:c1].rearrange("(p j) f -> p j f", j=4)
            nc.sync.dma_start(out=grad_rows[k][:, :, c0:c1], in_=view)

        def load_h(k, c0=0, c1=FEATURES):
            if k not in h_rows:
                h_rows[k] = stream.tile([P, 4, FEATURES], F32, name="h_rows", tag="h_rows", bufs=4, align_bytes=64)
            view = h_tokens[unit_rows(k), c0:c1].rearrange("(p j) f -> p j f", j=4)
            nc.sync.dma_start(out=h_rows[k][:, :, c0:c1], in_=view)

        def load_x(k):
            x_rows[k] = stream.tile([P, 4, FEATURES], BF16, name="x_rows", tag="x_rows", bufs=4, align_bytes=64)
            nc.sync.dma_start(out=x_rows[k][:], in_=x[unit_rows(k), :].rearrange("(p j) w -> p j w", j=4))

        def load_ahat(half):
            ahat_rows[half] = stream.tile([P, 4, NODES], BF16, name="ahat_rows", tag="ahat_rows", bufs=2, align_bytes=64)
            view = ahat[unit_rows(half), :].rearrange("(m t) j -> m t j", t=4)
            for pair in range(2):
                rows = slice(2 * pair, 2 * pair + 2)
                nc.sync.dma_start(out=ahat_rows[half][:, rows, :], in_=view[:, rows, :])

        def load_w():
            w_rows[0] = stream.tile([P, 4, FEATURES], BF16, name="w_rows", tag="w_rows", bufs=1, align_bytes=64)
            nc.sync.dma_start(out=w_rows[0][:], in_=gcn1_w.rearrange("(d p) f -> p d f", p=P))


        def transpose_two_tiles(key, tiles, pairs_of):
            bank = work_bank()
            for i in range(2):
                pairs = tiles[i].bitcast(F32)
                for u in range(2):
                    c0 = P * (2 * i + u)
                    nc.tensor.transpose(bank[:, c0 : c0 + P], pairs[:, pairs_of(u)], identity[:])
            banks[key] = bank

        def copy_transposed(key, name, pair):
            if name not in turned:
                turned[name] = stream.tile([P, UNIT, 4], BF16, name="turned", tag="turned", bufs=4, align_bytes=64)
            rows = turned[name][:, 2 * P * pair : 2 * P * (pair + 1), :].rearrange("q r v -> q (r v)")
            nc.scalar.copy(
                out=rows.bitcast(F32).rearrange("q (t r u) -> q t r u", t=2, u=2),
                in_=banks[key][:].rearrange("q (t u r) -> q t r u", t=2, u=2),
            )

        def every_second_pair(first):
            return lambda u: slice(first + u, first + HALF, 2)

        def side_by_side(u):
            return slice(P * u, P * (u + 1))


        def transpose_ahat(half, pair):
            tiles = [ahat_rows[half][:, 2 * pair + i, :] for i in range(2)]
            for s in range(2):
                transpose_two_tiles(("ahat", half, s, pair), tiles, every_second_pair(HALF * s))
                copy_transposed(("ahat", half, s, pair), ("ahat", half, s), pair)

        def quantize_ahat(half, pair):
            cols = slice(UNIT * half + 2 * P * pair, UNIT * half + 2 * P * (pair + 1))
            for s in range(2):
                values = turned["ahat", half, s][:, 2 * P * pair : 2 * P * (pair + 1), :]
                nc.vector.quantize_mx(
                    out=ahat_codes[s][:, cols].bitcast(E4M3),
                    scales=ahat_scales[s][:, cols],
                    in_=values.rearrange("q r v -> q (r v)"),
                )

        def transpose_w():
            for pair in range(2):
                tiles = [w_rows[0][:, 2 * pair + i, :] for i in range(2)]
                transpose_two_tiles(("w", pair), tiles, every_second_pair(0))
                copy_transposed(("w", pair), "w", pair)

        def quantize_w():
            nc.vector.quantize_mx(
                out=w_codes[:].bitcast(E4M3), scales=w_scales[:], in_=turned["w"][:].rearrange("q r v -> q (r v)")
            )


        def make_dz2(k, c0=0, c1=FEATURES):
            if k not in dz2_grouped:
                dz2_grouped[k] = stream.tile([P, FEATURES, 4], BF16, name="dz2_grouped", tag="dz2_grouped", bufs=3, align_bytes=64)
            nc.vector.scalar_tensor_tensor(
                out=dz2_grouped[k][:, c0:c1, :],
                in0=h_rows[k][:, :, c0:c1].rearrange("p j f -> p f j"),
                scalar=0.0,
                in1=grad_rows[k][:, :, c0:c1].rearrange("p j f -> p f j"),
                op0=ALU.is_gt,
                op1=ALU.mult,
            )

        def quantize_dz2(k):
            dz2_mx[k] = codes_and_scales("dz2", 4)
            codes, scales = dz2_mx[k]
            nc.vector.quantize_mx(
                out=codes[:].bitcast(E5M2), scales=scales[:], in_=dz2_grouped[k][:].rearrange("p f j -> p (f j)")
            )


        def multiply_dz1(k):
            half = k % 2
            for t in range(TILES):
                cols = slice(UNIT * half + P * t, UNIT * half + P * (t + 1))
                banks["dz1", k, t] = work_bank()
                for s in range(2):
                    codes, scales = dz2_mx[k - half + s]
                    nc.tensor.matmul_mx(
                        out=banks["dz1", k, t][:],
                        lhsT=ahat_codes[s][:, cols].bitcast(E4M3),
                        lhsT_scale=ahat_scales[s][:, cols],
                        rhs=codes[:].bitcast(E5M2),
                        rhs_scale=scales[:],
                        start=(s == 0),
                        stop=(s == 1),
                    )

        def copy_dz1(k):
            dz1[k] = stream.tile([P, TILES, FEATURES], BF16, name="dz1", tag="dz1", bufs=3, align_bytes=64)
            for t in range(TILES):
                nc.scalar.copy(
                    out=dz1[k][:, t, :].rearrange("p (u q e) -> p u q e", u=2, e=2),
                    in_=banks["dz1", k, t][:].rearrange("p (q u e) -> p u q e", u=2, e=2),
                )


        def group_dz1_tokens(k):
            dz1_grouped[k] = stream.tile([P, FEATURES, TILES], BF16, name="dz1_grouped", tag="dz1_grouped", bufs=2, align_bytes=64)
            nc.vector.tensor_copy(
                out=dz1_grouped[k][:].rearrange("p (c i) t -> p c t i", i=4),
                in_=dz1[k][:].rearrange("p t (c i) -> p c t i", i=4),
            )

        def quantize_dz1_tokens(k):
            dz1_token_mx[k] = codes_and_scales("dz1_token", 4)
            codes, scales = dz1_token_mx[k]
            nc.vector.quantize_mx(
                out=codes[:].bitcast(E5M2), scales=scales[:], in_=dz1_grouped[k][:].rearrange("p f t -> p (f t)")
            )

        def transpose_dz1(k):
            for pair in range(2):
                tiles = [dz1[k][:, 2 * pair + i, :] for i in range(2)]
                transpose_two_tiles(("dz1T", k, pair), tiles, side_by_side)
            for pair in range(2):
                copy_transposed(("dz1T", k, pair), ("dz1T", k), pair)

        def quantize_dz1_features(k):
            dz1_feature_mx[k] = codes_and_scales("dz1_feature", 2)
            codes, scales = dz1_feature_mx[k]
            nc.vector.quantize_mx(
                out=codes[:].bitcast(E5M2), scales=scales[:], in_=turned["dz1T", k][:].rearrange("q r v -> q (r v)")
            )


        def multiply_out_0(k):
            codes, scales = dz1_feature_mx[k]
            for t in range(TILES):
                cols = slice(P * t, P * (t + 1))
                banks["out_0", k, t] = work_bank()
                nc.tensor.matmul_mx(
                    out=banks["out_0", k, t][:],
                    lhsT=codes[:, cols].bitcast(E5M2),
                    lhsT_scale=scales[:, cols],
                    rhs=w_codes[:].bitcast(E4M3),
                    rhs_scale=w_scales[:],
                    start=True,
                    stop=True,
                )

        def store_out_0(k, pieces):
            out_0_rows[k] = stream.tile([P, TILES, FEATURES], F32, name="out_0_rows", tag="out_0_rows", bufs=3, align_bytes=64)
            view = out_0[unit_rows(k), :].rearrange("(p t) w -> p t w", t=TILES)
            step = TILES // pieces
            for t in range(TILES):
                nc.scalar.copy(out=out_0_rows[k][:, t, :], in_=banks["out_0", k, t][:])
                if (t + 1) % step == 0:
                    done = slice(t + 1 - step, t + 1)
                    nc.sync.dma_start(out=view[:, done, :], in_=out_0_rows[k][:, done, :])


        def group_x(k, c0, c1, copy):
            if k not in x_grouped:
                x_grouped[k] = stream.tile([P, FEATURES, 4], BF16, name="x_grouped", tag="x_grouped", bufs=2, align_bytes=64)
            copy(
                out=x_grouped[k][:, c0:c1, :].rearrange("p (c i) j -> p c j i", i=4),
                in_=x_rows[k][:, :, c0:c1].rearrange("p j (c i) -> p c j i", i=4),
            )

        def quantize_x(k):
            x_mx[k] = codes_and_scales("x", 4)
            codes, scales = x_mx[k]
            nc.vector.quantize_mx(
                out=codes[:].bitcast(E4M3), scales=scales[:], in_=x_grouped[k][:].rearrange("p w j -> p (w j)")
            )

        def multiply_out_1(k):
            x_codes, x_scales = x_mx[k]
            codes, scales = dz1_token_mx[k]
            for d in range(FEATURES // P):
                cols = slice(P * d, P * (d + 1))
                nc.tensor.matmul_mx(
                    out=out_1_banks[d][:],
                    lhsT=x_codes[:, cols].bitcast(E4M3),
                    lhsT_scale=x_scales[:, cols],
                    rhs=codes[:].bitcast(E5M2),
                    rhs_scale=scales[:],
                    start=(k == 0),
                    stop=(k == UNITS - 1),
                )

        def store_out_1():
            view = out_1.rearrange("(d p) f -> p d f", p=P)
            stores = {1: slice(0, 2), 2: slice(2, 3), 3: slice(3, 4)}
            for d in range(FEATURES // P):
                copy = nc.scalar.copy if d % 2 == 0 else nc.vector.tensor_copy
                copy(
                    out=out_1_rows[:, d, :].rearrange("p (q u e) -> p q u e", u=2, e=2),
                    in_=out_1_banks[d][:].rearrange("p (u q e) -> p q u e", u=2, e=2),
                )
                if d in stores:
                    nc.sync.dma_start(out=view[:, stores[d], :], in_=out_1_rows[:, stores[d], :])


        for c0 in range(0, FEATURES, HALF):
            load_grad(0, c0, c0 + HALF)
            load_h(0, c0, c0 + HALF)
        load_grad(1)
        load_h(1, 0, HALF)
        load_h(1, HALF, FEATURES)
        load_ahat(0)
        load_grad(2)
        load_h(2)
        load_ahat(1)
        load_w()
        load_x(0)
        load_grad(3)
        load_h(3)
        for k in range(1, 4):
            load_x(k)

        make_dz2(0, 0, HALF)
        make_dz2(0, HALF, FEATURES)
        load_grad(4)
        load_h(4)
        make_dz2(1, 0, HALF)
        quantize_dz2(0)
        make_dz2(1, HALF, FEATURES)
        load_grad(5)
        load_h(5)
        transpose_ahat(0, 0)
        transpose_ahat(0, 1)
        quantize_dz2(1)
        quantize_ahat(0, 0)
        quantize_ahat(0, 1)


        for k in range(UNITS - 2):
            multiply_dz1(k)
            copy_dz1(k)
            if k > 0:
                quantize_dz1_features(k - 1)
            make_dz2(k + 2)
            if k + 6 < UNITS:
                load_grad(k + 6)
                load_h(k + 6)
            if k == 0:
                transpose_dz1(k)
                transpose_ahat(1, 0)
                transpose_ahat(1, 1)
                transpose_w()
            else:
                group_x(k - 1, X_VECTOR_COLUMNS, FEATURES, nc.scalar.copy)
                multiply_out_0(k - 1)
                store_out_0(k - 1, 1)
                if k > 1:
                    multiply_out_1(k - 2)
                transpose_dz1(k)
            group_dz1_tokens(k)
            if k == 0:
                quantize_ahat(1, 0)
            quantize_dz2(k + 2)
            if k > 0:
                group_x(k - 1, 0, X_VECTOR_COLUMNS, nc.vector.tensor_copy)
            quantize_dz1_tokens(k)
            if k == 0:
                quantize_ahat(1, 1)
                quantize_w()
            else:
                quantize_x(k - 1)
                if k + 3 < UNITS:
                    load_x(k + 3)


        multiply_dz1(6)
        copy_dz1(6)
        quantize_dz1_features(5)
        group_x(5, 0, FEATURES, nc.vector.tensor_copy)
        multiply_out_1(4)
        multiply_out_0(5)
        store_out_0(5, 1)
        transpose_dz1(6)
        group_dz1_tokens(6)
        group_x(6, 0, FEATURES, nc.vector.tensor_copy)
        multiply_dz1(7)
        copy_dz1(7)
        quantize_dz1_tokens(6)
        quantize_dz1_features(6)
        quantize_x(5)
        transpose_dz1(7)
        group_dz1_tokens(7)
        multiply_out_0(6)
        store_out_0(6, 2)
        multiply_out_1(5)
        quantize_dz1_features(7)
        quantize_x(6)
        group_x(7, 0, FEATURES, nc.vector.tensor_copy)
        multiply_out_0(7)
        store_out_0(7, 2)
        quantize_dz1_tokens(7)
        multiply_out_1(6)
        quantize_x(7)
        multiply_out_1(7)
        store_out_1()
